import numpy as np
import ml_dtypes


def mxq(x, axis, fmt="e4m3"):
    dtype, down = {"e4m3": (ml_dtypes.float8_e4m3fn, 7), "e5m2": (ml_dtypes.float8_e5m2, 14)}[fmt]
    v = np.moveaxis(np.asarray(x, np.float32).astype(ml_dtypes.bfloat16).astype(np.float64), axis, -1)
    blocks = v.reshape(v.shape[:-1] + (-1, 32))
    amax = np.abs(blocks).max(-1, keepdims=True)
    byte = np.maximum(np.where(amax > 0, np.frexp(amax)[1] - 1 + 127, 0) - down, 1)
    scale = np.exp2(byte - 127.0)
    codes = (blocks / scale).astype(np.float32).astype(dtype).astype(np.float64)
    return np.moveaxis((codes * scale).reshape(v.shape), -1, axis)


WIDE = False


def mx_kscale(k):
    if not WIDE:
        return np.ones(k)
    levels = np.array([10, -10, 5, -5, 0])
    a = np.random.permutation(np.resize(levels, k // 512 * 4)).reshape(k // 512, 4)
    idx = np.arange(k)
    return np.exp2(a[idx // 512, idx % 128 // 32])


BF16 = ml_dtypes.bfloat16


def bf(x):
    return np.asarray(x, np.float32).astype(BF16)


def f64(x):
    return np.asarray(x).astype(np.float64)


E2M1 = np.array([0.0, 0.5, 1.0, 1.5, 2.0, 3.0, 4.0, 6.0, -0.0, -0.5, -1.0, -1.5, -2.0, -3.0, -4.0, -6.0])


def pack_weight(w, fmt):
    k, n = w.shape
    w = f64(bf(w)).reshape(k // 32, 32, n)
    amax = np.abs(w).max(1)
    if fmt == "e4m3":
        byte = np.frexp(amax)[1] - 1 + 127 - 7
    else:
        mant, ex = np.frexp(amax / 6.0)
        byte = np.where(mant > 0.5, ex, ex - 1) + 127
    byte = np.clip(np.where(amax > 0, byte, 1), 1, 254)
    scaled = (w * np.exp2(127.0 - byte)[:, None, :]).reshape(k, n).astype(np.float32)
    by_word = np.ascontiguousarray(scaled.reshape(k // 512, 128, 4, n).transpose(0, 1, 3, 2))
    if fmt == "e4m3":
        words = by_word.astype(ml_dtypes.float8_e4m3fn).view(np.uint8)
    else:
        c = by_word.astype(ml_dtypes.float4_e2m1fn).view(np.uint8) & 0xF
        words = c[..., 0::2] | (c[..., 1::2] << 4)
    return np.ascontiguousarray(words), np.ascontiguousarray(byte.astype(np.uint8).reshape(k // 512, 16, n))


def unpack_weight(words, scales, fmt):
    g, p, n, _ = words.shape
    if fmt == "e4m3":
        vals = np.ascontiguousarray(words).view(ml_dtypes.float8_e4m3fn).astype(np.float64)
    else:
        nib = np.empty((g, p, n, 4), np.uint8)
        nib[..., 0::2] = words & 0xF
        nib[..., 1::2] = words >> 4
        vals = E2M1[nib]
    vals = vals * np.repeat(np.exp2(scales.astype(np.float64) - 127.0), 8, axis=1)[..., None]
    return vals.transpose(0, 1, 3, 2).reshape(g * 512, n)


B, N, H, R, L = 2, 512, 512, 10, 2
NEG_INF = -1e30


def setup_inputs():
    s = mx_kscale(H)
    adj = bf(np.random.uniform(size=(B, N, N, R)) * 4.0)
    x = bf(np.random.standard_normal((B, N, H)) * s)
    dmask = bf(np.random.uniform(size=(B, 1, N)) > 0.1)
    stack = np.random.standard_normal((R, H, H)) * 1.5 / np.sqrt(H) / s[:, None]
    words, scales = pack_weight(stack.reshape(-1, H), "e4m3")
    return {"adj": adj,
            "x": x,
            "dmask": dmask,
            "W_words": words,
            "W_scales": scales}


def reference(adj, x, dmask, W_words, W_scales):
    a = f64(adj).transpose(0, 3, 1, 2)
    m = f64(dmask)[:, None, :, :]
    logits = a * m + (1.0 - m) * NEG_INF
    e = np.exp(logits - logits.max(-1, keepdims=True))
    att = e / e.sum(-1, keepdims=True)
    h = mxq(f64(x), 2, "e4m3")[:, None] @ unpack_weight(W_words, W_scales, "e4m3").reshape(R, H, H)[None]
    g = np.maximum(mxq(att, 3, "e4m3") @ mxq(h, 2, "e4m3"), 0.0)
    return g.sum(1)

@@ -1,0 +1,283 @@
+from contextlib import ExitStack
+
+import concourse.mybir as mybir
+from concourse.masks import make_identity
+
+F32 = mybir.dt.float32
+BF16 = mybir.dt.bfloat16
+I32 = mybir.dt.int32
+U32 = mybir.dt.uint32
+U8 = mybir.dt.uint8
+FP8X4 = mybir.dt.float8_e4m3fn_x4
+ALU = mybir.AluOpType
+ACT = mybir.ActivationFunctionType
+
+P = 128
+PACK = 4
+GRAPHS = 2
+NODES = 512
+FEATS = 512
+RELS = 10
+PAIRS = RELS // 2
+NODE_TILES = NODES // P
+TILES = GRAPHS * NODE_TILES
+NEG_INF = -1e30
+BF16_MAX = 3.3895313892515355e38
+FOLDS = 4
+PROJECTIONS_PER_STEP = 5
+
+FLOPS = 2 * 2 * GRAPHS * RELS * NODES * NODES * FEATS
+
+
+def tile_rgat_pa_e_kernel(tc, adj, x, dmask, W_words, W_scales, out):
+    nc = tc.nc
+    with ExitStack() as stack:
+        keep = stack.enter_context(tc.tile_pool(name="keep", bufs=1))
+        turned_banks = stack.enter_context(tc.psum_pool(name="turned_banks", bufs=2))
+        h_banks = stack.enter_context(tc.psum_pool(name="h_banks", bufs=3))
+        z_banks = stack.enter_context(tc.psum_pool(name="z_banks", bufs=3))
+
+        ident = keep.tile([P, P], F32, name="ident")
+        make_identity(nc, ident[:])
+
+        ceiling = keep.tile([P, GRAPHS, NODES, 2], BF16, name="ceiling")
+        w_words = keep.tile([P, RELS, FEATS], U32, name="w_words", align_bytes=64)
+        w_planes = keep.tile([P, RELS, FEATS], U8, name="w_planes", align_bytes=64)
+        x_codes = keep.tile([P, GRAPHS, NODES], U32, name="x_codes", align_bytes=64)
+        x_planes = keep.tile([P, GRAPHS, NODES], U8, name="x_planes", align_bytes=64)
+        h_codes = {}
+        h_planes = {}
+        for b in range(GRAPHS):
+            for r in range(RELS):
+                h_codes[(b, r)] = keep.tile([P, FEATS], U32, name="h_codes_%d_%d" % (b, r), align_bytes=64)
+                h_planes[(b, r)] = keep.tile([P, FEATS], U8, name="h_planes_%d_%d" % (b, r), align_bytes=64)
+
+        nc.vector.memset(w_planes[:].bitcast(I32), 0)
+
+        score_pool = stack.enter_context(tc.tile_pool(name="score_pool", bufs=2))
+        scores = {}
+
+        def load_scores(i):
+            b, t = divmod(i, NODE_TILES)
+            scores[i] = score_pool.tile([P, NODES * RELS], BF16, name="scores")
+            nc.sync.dma_start(
+                out=scores[i][:],
+                in_=adj[b, t * P : (t + 1) * P].rearrange("n m r -> n (m r)"),
+            )
+
+        with tc.tile_pool(name="start", bufs=2) as start:
+            mask_rows = start.tile([P, GRAPHS * NODES], BF16, name="mask_rows", bufs=1)
+            nc.sync.dma_start(
+                out=mask_rows[:],
+                in_=dmask.rearrange("b o m -> (b o m)").partition_broadcast(P),
+            )
+            load_scores(0)
+            x_rows = {}
+            for b in range(GRAPHS):
+                x_rows[b] = start.tile([P, PACK, FEATS], BF16, name="x_rows")
+            nc.sync.dma_start(out=x_rows[0][:], in_=x[0].rearrange("(p t) f -> p t f", t=PACK))
+            for q in range(4):
+                nc.sync.dma_start(
+                    out=w_planes[32 * q : 32 * q + 4].bitcast(I32),
+                    in_=W_scales[:, 4 * q : 4 * q + 4, :].rearrange("g s n -> s g n").bitcast(I32),
+                )
+            words_in_dram = W_words.rearrange("g p n t -> p g (n t)").bitcast(I32)
+            nc.sync.dma_start(out=w_words[:, 0:5, :].bitcast(I32), in_=words_in_dram[:, 0:5, :])
+            load_scores(1)
+            nc.sync.dma_start(out=x_rows[1][:], in_=x[1].rearrange("(p t) f -> p t f", t=PACK))
+            nc.sync.dma_start(out=w_words[:, 5:10, :].bitcast(I32), in_=words_in_dram[:, 5:10, :])
+
+            nc.vector.tensor_scalar(
+                out=ceiling[:],
+                in0=mask_rows[:]
+                .rearrange("p (b m) -> p b m", b=GRAPHS)
+                .unsqueeze(3)
+                .to_broadcast([P, GRAPHS, NODES, 2]),
+                scalar1=BF16_MAX,
+                scalar2=NEG_INF,
+                op0=ALU.mult,
+                op1=ALU.add,
+            )
+
+            for b in range(GRAPHS):
+                x_as_words = x_rows[b][:].bitcast(F32)
+                x_grouped = start.tile([P, PACK, P, PACK], BF16, name="x_grouped", align_bytes=64)
+                for half in range(2):
+                    turned = turned_banks.tile([P, 2, 2, P], F32, name="turned")
+                    for s in range(2):
+                        for u in range(2):
+                            nc.tensor.transpose(
+                                turned[:, s, u, :],
+                                x_as_words[:, 2 * half + s, u : FEATS // 2 : 2],
+                                ident[:],
+                            )
+                    nc.scalar.copy(
+                        out=x_grouped[:, 2 * half : 2 * half + 2].bitcast(F32),
+                        in_=turned[:].rearrange("q s u n -> q s n u"),
+                    )
+                nc.vector.quantize_mx(
+                    out=x_codes[:, b, :].bitcast(FP8X4),
+                    scales=x_planes[:, b, :],
+                    in_=x_grouped[:].rearrange("q t n k -> q (t n k)"),
+                )
+
+        exp_pool = stack.enter_context(tc.tile_pool(name="exp_pool", bufs=2))
+        masked_pool = stack.enter_context(tc.tile_pool(name="masked_pool", bufs=2))
+        fold_pool = stack.enter_context(tc.tile_pool(name="fold_pool", bufs=1))
+        stat_pool = stack.enter_context(tc.tile_pool(name="stat_pool", bufs=3))
+        att_pool = stack.enter_context(tc.tile_pool(name="att_pool", bufs=4))
+        code_pool = stack.enter_context(tc.tile_pool(name="code_pool", bufs=3))
+        h_pool = stack.enter_context(tc.tile_pool(name="h_pool", bufs=2))
+        out_pool = stack.enter_context(tc.tile_pool(name="out_pool", bufs=2))
+
+        masked = {}
+        neg_max = {}
+        exps = {}
+        inv_sum = {}
+        att_codes = {}
+        att_planes = {}
+
+        def mask_and_max(i):
+            b = i // NODE_TILES
+            masked[i] = masked_pool.tile([P, PAIRS, NODES, 2], BF16, name="masked")
+            nc.vector.tensor_tensor(
+                out=masked[i][:],
+                in0=scores[i][:].rearrange("p (m j e) -> p j m e", j=PAIRS, e=2),
+                in1=ceiling[:, b].unsqueeze(1).to_broadcast([P, PAIRS, NODES, 2]),
+                op=ALU.min,
+            )
+            level = masked[i][:].rearrange("p j m e -> p j (m e)")
+            width = NODES * 2
+            for depth in range(FOLDS):
+                width //= 2
+                folded = fold_pool.tile([P, PAIRS, width], BF16, name="folded_%d" % depth)
+                nc.vector.tensor_tensor(
+                    out=folded[:],
+                    in0=level[:, :, 0:width],
+                    in1=level[:, :, width : 2 * width],
+                    op=ALU.max,
+                )
+                level = folded[:]
+            neg_max[i] = stat_pool.tile([P, RELS], F32, name="neg_max")
+            nc.vector.tensor_reduce(
+                out=neg_max[i][:].rearrange("p (j e) -> p j e", e=2),
+                in_=level.rearrange("p j (m e) -> p j e m", e=2),
+                axis=mybir.AxisListType.X,
+                op=ALU.max,
+                negate=True,
+            )
+
+        def exponentials(i):
+            exps[i] = exp_pool.tile([P, RELS, NODES], F32, name="exps")
+            sums = stat_pool.tile([P, RELS], F32, name="sums")
+            for r in range(RELS):
+                nc.scalar.activation(
+                    out=exps[i][:, r, :],
+                    in_=masked[i][:, r // 2, :, r % 2],
+                    func=ACT.Exp,
+                    bias=neg_max[i][:, r : r + 1],
+                    scale=1.0,
+                    accum_out=sums[:, r : r + 1],
+                )
+            inv_sum[i] = stat_pool.tile([P, RELS], F32, name="inv_sum")
+            nc.vector.reciprocal(out=inv_sum[i][:], in_=sums[:])
+
+        def attend(i):
+            att_codes[i] = code_pool.tile([P, RELS, P], U32, name="att_codes", align_bytes=64)
+            att_planes[i] = code_pool.tile([P, RELS, P], U8, name="att_planes", align_bytes=64)
+            for j in range(PAIRS):
+                att = att_pool.tile([P, 2, NODES], BF16, name="att")
+                for e in range(2):
+                    r = 2 * j + e
+                    nc.vector.tensor_scalar(
+                        out=att[:, e, :],
+                        in0=exps[i][:, r, :],
+                        scalar1=inv_sum[i][:, r : r + 1],
+                        scalar2=None,
+                        op0=ALU.mult,
+                    )
+                att_as_words = att[:].bitcast(F32)
+                turned = turned_banks.tile([P, 2, 2, P], F32, name="turned")
+                for e in range(2):
+                    for u in range(2):
+                        nc.tensor.transpose(
+                            turned[:, e, u, :],
+                            att_as_words[:, e, u : NODES // 2 : 2],
+                            ident[:],
+                        )
+                att_grouped = att_pool.tile([P, 2, P, PACK], BF16, name="att_grouped", align_bytes=64)
+                nc.scalar.copy(
+                    out=att_grouped[:].bitcast(F32),
+                    in_=turned[:].rearrange("q e u n -> q e n u"),
+                )
+                nc.vector.quantize_mx(
+                    out=att_codes[i][:, 2 * j : 2 * j + 2, :].rearrange("q e n -> q (e n)").bitcast(FP8X4),
+                    scales=att_planes[i][:, 2 * j : 2 * j + 2, :].rearrange("q e n -> q (e n)"),
+                    in_=att_grouped[:].rearrange("q e n k -> q (e n k)"),
+                )
+
+        def project(b, r):
+            h_grouped = h_pool.tile([P, FEATS, PACK], BF16, name="h_grouped", align_bytes=64)
+            for c in range(FEATS // P):
+                cols = slice(c * P, (c + 1) * P)
+                h_bank = h_banks.tile([P, PACK, P], F32, name="h_bank")
+                for t in range(PACK):
+                    nodes = slice(t * P, (t + 1) * P)
+                    nc.tensor.matmul_mx(
+                        out=h_bank[:, t, :],
+                        lhsT=x_codes[:, b, nodes].bitcast(FP8X4),
+                        lhsT_scale=x_planes[:, b, nodes],
+                        rhs=w_words[:, r, cols].bitcast(FP8X4),
+                        rhs_scale=w_planes[:, r, cols],
+                        start=True,
+                        stop=True,
+                    )
+                nc.scalar.copy(out=h_grouped[:, cols, :], in_=h_bank[:].rearrange("p t w -> p w t"))
+            nc.vector.quantize_mx(
+                out=h_codes[(b, r)][:].bitcast(FP8X4),
+                scales=h_planes[(b, r)][:],
+                in_=h_grouped[:].rearrange("p w t -> p (w t)"),
+            )
+
+        def aggregate(i):
+            b, t = divmod(i, NODE_TILES)
+            total = out_pool.tile([P, FEATS], F32, name="total")
+            for r in range(RELS):
+                z_bank = z_banks.tile([P, FEATS], F32, name="z_bank")
+                nc.tensor.matmul_mx(
+                    out=z_bank[:],
+                    lhsT=att_codes[i][:, r, :].bitcast(FP8X4),
+                    lhsT_scale=att_planes[i][:, r, :],
+                    rhs=h_codes[(b, r)][:].bitcast(FP8X4),
+                    rhs_scale=h_planes[(b, r)][:],
+                    start=True,
+                    stop=True,
+                )
+                if r == 0:
+                    nc.scalar.activation(out=total[:], in_=z_bank[:], func=ACT.Relu)
+                else:
+                    nc.vector.scalar_tensor_tensor(
+                        out=total[:],
+                        in0=z_bank[:],
+                        scalar=0.0,
+                        in1=total[:],
+                        op0=ALU.max,
+                        op1=ALU.add,
+                    )
+            nc.sync.dma_start(out=out[b, t * P : (t + 1) * P, :], in_=total[:])
+
+        projections = [(b, r) for b in range(GRAPHS) for r in range(RELS)]
+        mask_and_max(0)
+        for i in range(TILES + 1):
+            if i < TILES:
+                exponentials(i)
+            if i + 2 < TILES:
+                load_scores(i + 2)
+            if i + 1 < TILES:
+                mask_and_max(i + 1)
+            if i < TILES:
+                attend(i)
+            for b, r in projections[i * PROJECTIONS_PER_STEP : (i + 1) * PROJECTIONS_PER_STEP]:
+                project(b, r)
+            if i >= 1:
+                aggregate(i - 1)

@@ -24,7 +24,9 @@ TILES = GRAPHS * NODE_TILES
 NEG_INF = -1e30
 BF16_MAX = 3.3895313892515355e38
 FOLDS = 4
-PROJECTIONS_PER_STEP = 5
+H_BANKS = GRAPHS * RELS * (FEATS // P)
+H_BANKS_PER_TICK = 2
+X_TICK = 1
 
 FLOPS = 2 * 2 * GRAPHS * RELS * NODES * NODES * FEATS
 
@@ -32,14 +34,25 @@ FLOPS = 2 * 2 * GRAPHS * RELS * NODES * NODES * FEATS
 def tile_rgat_pa_e_kernel(tc, adj, x, dmask, W_words, W_scales, out):
     nc = tc.nc
     with ExitStack() as stack:
+        stack.enter_context(tc.manual_schedule())
         keep = stack.enter_context(tc.tile_pool(name="keep", bufs=1))
         turned_banks = stack.enter_context(tc.psum_pool(name="turned_banks", bufs=2))
         h_banks = stack.enter_context(tc.psum_pool(name="h_banks", bufs=3))
         z_banks = stack.enter_context(tc.psum_pool(name="z_banks", bufs=3))
+        score_pool = stack.enter_context(tc.tile_pool(name="score_pool", bufs=2))
+        masked_pool = stack.enter_context(tc.tile_pool(name="masked_pool", bufs=3))
+        fold_pool = stack.enter_context(tc.tile_pool(name="fold_pool", bufs=1))
+        stat_pool = stack.enter_context(tc.tile_pool(name="stat_pool", bufs=3))
+        exp_pool = stack.enter_context(tc.tile_pool(name="exp_pool", bufs=2))
+        att_pool = stack.enter_context(tc.tile_pool(name="att_pool", bufs=3))
+        code_pool = stack.enter_context(tc.tile_pool(name="code_pool", bufs=2))
+        h_pool = stack.enter_context(tc.tile_pool(name="h_pool", bufs=2))
+        out_pool = stack.enter_context(tc.tile_pool(name="out_pool", bufs=2))
 
         ident = keep.tile([P, P], F32, name="ident")
         make_identity(nc, ident[:])
 
+        mask_rows = keep.tile([P, GRAPHS * NODES], BF16, name="mask_rows")
         ceiling = keep.tile([P, GRAPHS, NODES, 2], BF16, name="ceiling")
         w_words = keep.tile([P, RELS, FEATS], U32, name="w_words", align_bytes=64)
         w_planes = keep.tile([P, RELS, FEATS], U8, name="w_planes", align_bytes=64)
@@ -52,10 +65,20 @@ def tile_rgat_pa_e_kernel(tc, adj, x, dmask, W_words, W_scales, out):
                 h_codes[(b, r)] = keep.tile([P, FEATS], U32, name="h_codes_%d_%d" % (b, r), align_bytes=64)
                 h_planes[(b, r)] = keep.tile([P, FEATS], U8, name="h_planes_%d_%d" % (b, r), align_bytes=64)
 
-        nc.vector.memset(w_planes[:].bitcast(I32), 0)
-
-        score_pool = stack.enter_context(tc.tile_pool(name="score_pool", bufs=2))
         scores = {}
+        masked = {}
+        folded = {}
+        neg_max = {}
+        exps = {}
+        sums = {}
+        inv_sum = {}
+        att = {}
+        att_grouped = {}
+        att_codes = {}
+        att_planes = {}
+        h_grouped = {}
+        z_bank = {}
+        total = {}
 
         def load_scores(i):
             b, t = divmod(i, NODE_TILES)
@@ -65,160 +88,92 @@ def tile_rgat_pa_e_kernel(tc, adj, x, dmask, W_words, W_scales, out):
                 in_=adj[b, t * P : (t + 1) * P].rearrange("n m r -> n (m r)"),
             )
 
-        with tc.tile_pool(name="start", bufs=2) as start:
-            mask_rows = start.tile([P, GRAPHS * NODES], BF16, name="mask_rows", bufs=1)
-            nc.sync.dma_start(
-                out=mask_rows[:],
-                in_=dmask.rearrange("b o m -> (b o m)").partition_broadcast(P),
-            )
-            load_scores(0)
-            x_rows = {}
-            for b in range(GRAPHS):
-                x_rows[b] = start.tile([P, PACK, FEATS], BF16, name="x_rows")
-            nc.sync.dma_start(out=x_rows[0][:], in_=x[0].rearrange("(p t) f -> p t f", t=PACK))
-            for q in range(4):
-                nc.sync.dma_start(
-                    out=w_planes[32 * q : 32 * q + 4].bitcast(I32),
-                    in_=W_scales[:, 4 * q : 4 * q + 4, :].rearrange("g s n -> s g n").bitcast(I32),
-                )
-            words_in_dram = W_words.rearrange("g p n t -> p g (n t)").bitcast(I32)
-            nc.sync.dma_start(out=w_words[:, 0:5, :].bitcast(I32), in_=words_in_dram[:, 0:5, :])
-            load_scores(1)
-            nc.sync.dma_start(out=x_rows[1][:], in_=x[1].rearrange("(p t) f -> p t f", t=PACK))
-            nc.sync.dma_start(out=w_words[:, 5:10, :].bitcast(I32), in_=words_in_dram[:, 5:10, :])
-
-            nc.vector.tensor_scalar(
-                out=ceiling[:],
-                in0=mask_rows[:]
-                .rearrange("p (b m) -> p b m", b=GRAPHS)
-                .unsqueeze(3)
-                .to_broadcast([P, GRAPHS, NODES, 2]),
-                scalar1=BF16_MAX,
-                scalar2=NEG_INF,
-                op0=ALU.mult,
-                op1=ALU.add,
-            )
-
-            for b in range(GRAPHS):
-                x_as_words = x_rows[b][:].bitcast(F32)
-                x_grouped = start.tile([P, PACK, P, PACK], BF16, name="x_grouped", align_bytes=64)
-                for half in range(2):
-                    turned = turned_banks.tile([P, 2, 2, P], F32, name="turned")
-                    for s in range(2):
-                        for u in range(2):
-                            nc.tensor.transpose(
-                                turned[:, s, u, :],
-                                x_as_words[:, 2 * half + s, u : FEATS // 2 : 2],
-                                ident[:],
-                            )
-                    nc.scalar.copy(
-                        out=x_grouped[:, 2 * half : 2 * half + 2].bitcast(F32),
-                        in_=turned[:].rearrange("q s u n -> q s n u"),
-                    )
-                nc.vector.quantize_mx(
-                    out=x_codes[:, b, :].bitcast(FP8X4),
-                    scales=x_planes[:, b, :],
-                    in_=x_grouped[:].rearrange("q t n k -> q (t n k)"),
-                )
-
-        exp_pool = stack.enter_context(tc.tile_pool(name="exp_pool", bufs=2))
-        masked_pool = stack.enter_context(tc.tile_pool(name="masked_pool", bufs=2))
-        fold_pool = stack.enter_context(tc.tile_pool(name="fold_pool", bufs=1))
-        stat_pool = stack.enter_context(tc.tile_pool(name="stat_pool", bufs=3))
-        att_pool = stack.enter_context(tc.tile_pool(name="att_pool", bufs=4))
-        code_pool = stack.enter_context(tc.tile_pool(name="code_pool", bufs=3))
-        h_pool = stack.enter_context(tc.tile_pool(name="h_pool", bufs=2))
-        out_pool = stack.enter_context(tc.tile_pool(name="out_pool", bufs=2))
-
-        masked = {}
-        neg_max = {}
-        exps = {}
-        inv_sum = {}
-        att_codes = {}
-        att_planes = {}
-
-        def mask_and_max(i):
+        def mask_scores(i, j):
             b = i // NODE_TILES
-            masked[i] = masked_pool.tile([P, PAIRS, NODES, 2], BF16, name="masked")
+            if j == 0:
+                masked[i] = masked_pool.tile([P, PAIRS, NODES, 2], BF16, name="masked")
             nc.vector.tensor_tensor(
-                out=masked[i][:],
-                in0=scores[i][:].rearrange("p (m j e) -> p j m e", j=PAIRS, e=2),
-                in1=ceiling[:, b].unsqueeze(1).to_broadcast([P, PAIRS, NODES, 2]),
+                out=masked[i][:, j],
+                in0=scores[i][:].rearrange("p (m j e) -> p j m e", j=PAIRS, e=2)[:, j],
+                in1=ceiling[:, b],
                 op=ALU.min,
             )
-            level = masked[i][:].rearrange("p j m e -> p j (m e)")
-            width = NODES * 2
-            for depth in range(FOLDS):
-                width //= 2
-                folded = fold_pool.tile([P, PAIRS, width], BF16, name="folded_%d" % depth)
+
+        def fold_maxima(i, depth):
+            if depth < FOLDS:
+                wide = masked[i][:].rearrange("p j m e -> p j (m e)") if depth == 0 else folded[i][:]
+                width = NODES >> depth
+                folded[i] = fold_pool.tile([P, PAIRS, width], BF16, name="folded_%d" % depth)
                 nc.vector.tensor_tensor(
-                    out=folded[:],
-                    in0=level[:, :, 0:width],
-                    in1=level[:, :, width : 2 * width],
+                    out=folded[i][:],
+                    in0=wide[:, :, 0:width],
+                    in1=wide[:, :, width : 2 * width],
                     op=ALU.max,
                 )
-                level = folded[:]
-            neg_max[i] = stat_pool.tile([P, RELS], F32, name="neg_max")
-            nc.vector.tensor_reduce(
-                out=neg_max[i][:].rearrange("p (j e) -> p j e", e=2),
-                in_=level.rearrange("p j (m e) -> p j e m", e=2),
-                axis=mybir.AxisListType.X,
-                op=ALU.max,
-                negate=True,
+            else:
+                neg_max[i] = stat_pool.tile([P, RELS], F32, name="neg_max")
+                nc.vector.tensor_reduce(
+                    out=neg_max[i][:].rearrange("p (j e) -> p j e", e=2),
+                    in_=folded[i][:].rearrange("p j (m e) -> p j e m", e=2),
+                    axis=mybir.AxisListType.X,
+                    op=ALU.max,
+                    negate=True,
+                )
+
+        def exponential(i, r):
+            if r == 0:
+                exps[i] = exp_pool.tile([P, RELS, NODES], F32, name="exps")
+                sums[i] = stat_pool.tile([P, RELS], F32, name="sums")
+            nc.scalar.activation(
+                out=exps[i][:, r, :],
+                in_=masked[i][:, r // 2, :, r % 2],
+                func=ACT.Exp,
+                bias=neg_max[i][:, r : r + 1],
+                scale=1.0,
+                accum_out=sums[i][:, r : r + 1],
             )
 
-        def exponentials(i):
-            exps[i] = exp_pool.tile([P, RELS, NODES], F32, name="exps")
-            sums = stat_pool.tile([P, RELS], F32, name="sums")
-            for r in range(RELS):
-                nc.scalar.activation(
-                    out=exps[i][:, r, :],
-                    in_=masked[i][:, r // 2, :, r % 2],
-                    func=ACT.Exp,
-                    bias=neg_max[i][:, r : r + 1],
-                    scale=1.0,
-                    accum_out=sums[:, r : r + 1],
-                )
+        def invert_sums(i):
             inv_sum[i] = stat_pool.tile([P, RELS], F32, name="inv_sum")
-            nc.vector.reciprocal(out=inv_sum[i][:], in_=sums[:])
-
-        def attend(i):
+            nc.vector.reciprocal(out=inv_sum[i][:], in_=sums[i][:])
             att_codes[i] = code_pool.tile([P, RELS, P], U32, name="att_codes", align_bytes=64)
             att_planes[i] = code_pool.tile([P, RELS, P], U8, name="att_planes", align_bytes=64)
-            for j in range(PAIRS):
-                att = att_pool.tile([P, 2, NODES], BF16, name="att")
-                for e in range(2):
-                    r = 2 * j + e
-                    nc.vector.tensor_scalar(
-                        out=att[:, e, :],
-                        in0=exps[i][:, r, :],
-                        scalar1=inv_sum[i][:, r : r + 1],
-                        scalar2=None,
-                        op0=ALU.mult,
-                    )
-                att_as_words = att[:].bitcast(F32)
-                turned = turned_banks.tile([P, 2, 2, P], F32, name="turned")
-                for e in range(2):
-                    for u in range(2):
-                        nc.tensor.transpose(
-                            turned[:, e, u, :],
-                            att_as_words[:, e, u : NODES // 2 : 2],
-                            ident[:],
-                        )
-                att_grouped = att_pool.tile([P, 2, P, PACK], BF16, name="att_grouped", align_bytes=64)
-                nc.scalar.copy(
-                    out=att_grouped[:].bitcast(F32),
-                    in_=turned[:].rearrange("q e u n -> q e n u"),
-                )
-                nc.vector.quantize_mx(
-                    out=att_codes[i][:, 2 * j : 2 * j + 2, :].rearrange("q e n -> q (e n)").bitcast(FP8X4),
-                    scales=att_planes[i][:, 2 * j : 2 * j + 2, :].rearrange("q e n -> q (e n)"),
-                    in_=att_grouped[:].rearrange("q e n k -> q (e n k)"),
-                )
 
-        def project(b, r):
-            h_grouped = h_pool.tile([P, FEATS, PACK], BF16, name="h_grouped", align_bytes=64)
-            for c in range(FEATS // P):
+        def normalise(i, r):
+            if r % 2 == 0:
+                att[i] = att_pool.tile([P, 2, NODES], BF16, name="att")
+            nc.vector.tensor_scalar(
+                out=att[i][:, r % 2, :],
+                in0=exps[i][:, r, :],
+                scalar1=inv_sum[i][:, r : r + 1],
+                scalar2=None,
+                op0=ALU.mult,
+            )
+
+        def turn(rows, grouped):
+            rows_as_words = rows.bitcast(F32)
+            turned = turned_banks.tile([P, 2, 2, P], F32, name="turned")
+            for e in range(2):
+                for u in range(2):
+                    nc.tensor.transpose(turned[:, e, u, :], rows_as_words[:, e, u : NODES // 2 : 2], ident[:])
+            nc.scalar.copy(out=grouped.bitcast(F32), in_=turned[:].rearrange("q e u n -> q e n u"))
+
+        def turn_att(i, j):
+            att_grouped[(i, j)] = att_pool.tile([P, 2, P, PACK], BF16, name="att_grouped", align_bytes=64)
+            turn(att[i][:], att_grouped[(i, j)][:])
+
+        def quantise_att(i, j):
+            nc.vector.quantize_mx(
+                out=att_codes[i][:, 2 * j : 2 * j + 2, :].rearrange("q e n -> q (e n)").bitcast(FP8X4),
+                scales=att_planes[i][:, 2 * j : 2 * j + 2, :].rearrange("q e n -> q (e n)"),
+                in_=att_grouped[(i, j)][:].rearrange("q e n k -> q (e n k)"),
+            )
+
+        def project(first_bank, last_bank):
+            for k in range(first_bank, min(last_bank, H_BANKS)):
+                b, r, c = k // (4 * RELS), (k // 4) % RELS, k % 4
+                if c == 0:
+                    h_grouped[(b, r)] = h_pool.tile([P, FEATS, PACK], BF16, name="h_grouped", align_bytes=64)
                 cols = slice(c * P, (c + 1) * P)
                 h_bank = h_banks.tile([P, PACK, P], F32, name="h_bank")
                 for t in range(PACK):
@@ -232,52 +187,136 @@ def tile_rgat_pa_e_kernel(tc, adj, x, dmask, W_words, W_scales, out):
                         start=True,
                         stop=True,
                     )
-                nc.scalar.copy(out=h_grouped[:, cols, :], in_=h_bank[:].rearrange("p t w -> p w t"))
-            nc.vector.quantize_mx(
-                out=h_codes[(b, r)][:].bitcast(FP8X4),
-                scales=h_planes[(b, r)][:],
-                in_=h_grouped[:].rearrange("p w t -> p (w t)"),
+                nc.scalar.copy(out=h_grouped[(b, r)][:, cols, :], in_=h_bank[:].rearrange("p t w -> p w t"))
+            return min(last_bank, H_BANKS)
+
+        def quantise_h(first_bank, last_bank):
+            for unit in range(first_bank // 4, last_bank // 4):
+                b, r = divmod(unit, RELS)
+                nc.vector.quantize_mx(
+                    out=h_codes[(b, r)][:].bitcast(FP8X4),
+                    scales=h_planes[(b, r)][:],
+                    in_=h_grouped[(b, r)][:].rearrange("p w t -> p (w t)"),
+                )
+            return last_bank
+
+        def multiply(i, r):
+            b = i // NODE_TILES
+            z_bank[(i, r)] = z_banks.tile([P, FEATS], F32, name="z_bank")
+            nc.tensor.matmul_mx(
+                out=z_bank[(i, r)][:],
+                lhsT=att_codes[i][:, r, :].bitcast(FP8X4),
+                lhsT_scale=att_planes[i][:, r, :],
+                rhs=h_codes[(b, r)][:].bitcast(FP8X4),
+                rhs_scale=h_planes[(b, r)][:],
+                start=True,
+                stop=True,
             )
 
-        def aggregate(i):
-            b, t = divmod(i, NODE_TILES)
-            total = out_pool.tile([P, FEATS], F32, name="total")
-            for r in range(RELS):
-                z_bank = z_banks.tile([P, FEATS], F32, name="z_bank")
-                nc.tensor.matmul_mx(
-                    out=z_bank[:],
-                    lhsT=att_codes[i][:, r, :].bitcast(FP8X4),
-                    lhsT_scale=att_planes[i][:, r, :],
-                    rhs=h_codes[(b, r)][:].bitcast(FP8X4),
-                    rhs_scale=h_planes[(b, r)][:],
-                    start=True,
-                    stop=True,
+        def add_relu(i, r):
+            if r == 0:
+                total[i] = out_pool.tile([P, FEATS], F32, name="total")
+                nc.scalar.activation(out=total[i][:], in_=z_bank[(i, r)][:], func=ACT.Relu)
+            else:
+                nc.vector.scalar_tensor_tensor(
+                    out=total[i][:],
+                    in0=z_bank[(i, r)][:],
+                    scalar=0.0,
+                    in1=total[i][:],
+                    op0=ALU.max,
+                    op1=ALU.add,
                 )
-                if r == 0:
-                    nc.scalar.activation(out=total[:], in_=z_bank[:], func=ACT.Relu)
-                else:
-                    nc.vector.scalar_tensor_tensor(
-                        out=total[:],
-                        in0=z_bank[:],
-                        scalar=0.0,
-                        in1=total[:],
-                        op0=ALU.max,
-                        op1=ALU.add,
-                    )
-            nc.sync.dma_start(out=out[b, t * P : (t + 1) * P, :], in_=total[:])
 
-        projections = [(b, r) for b in range(GRAPHS) for r in range(RELS)]
-        mask_and_max(0)
-        for i in range(TILES + 1):
-            if i < TILES:
-                exponentials(i)
-            if i + 2 < TILES:
-                load_scores(i + 2)
-            if i + 1 < TILES:
-                mask_and_max(i + 1)
-            if i < TILES:
-                attend(i)
-            for b, r in projections[i * PROJECTIONS_PER_STEP : (i + 1) * PROJECTIONS_PER_STEP]:
-                project(b, r)
-            if i >= 1:
-                aggregate(i - 1)
+        def store(i):
+            b, t = divmod(i, NODE_TILES)
+            nc.sync.dma_start(out=out[b, t * P : (t + 1) * P, :], in_=total[i][:])
+
+        nc.vector.memset(w_planes[:].bitcast(I32), 0)
+        nc.scalar.dma_start(
+            out=mask_rows[:],
+            in_=dmask.rearrange("b o m -> (b o m)").partition_broadcast(P),
+        )
+        load_scores(0)
+        x_rows = {}
+        for b in range(GRAPHS):
+            x_rows[b] = exp_pool.tile([P, PACK, FEATS], BF16, name="x_rows", tag="exps")
+            nc.sync.dma_start(out=x_rows[b][:], in_=x[b].rearrange("(p t) f -> p t f", t=PACK))
+        for q in range(4):
+            nc.sync.dma_start(
+                out=w_planes[32 * q : 32 * q + 4].bitcast(I32),
+                in_=W_scales[:, 4 * q : 4 * q + 4, :].rearrange("g s n -> s g n").bitcast(I32),
+            )
+        words_in_dram = W_words.rearrange("g p n t -> p g (n t)").bitcast(I32)
+        nc.sync.dma_start(out=w_words[:, 0:2, :].bitcast(I32), in_=words_in_dram[:, 0:2, :])
+        nc.sync.dma_start(out=w_words[:, 2:5, :].bitcast(I32), in_=words_in_dram[:, 2:5, :])
+        load_scores(1)
+        nc.sync.dma_start(out=w_words[:, 5:10, :].bitcast(I32), in_=words_in_dram[:, 5:10, :])
+
+        nc.vector.tensor_scalar(
+            out=ceiling[:],
+            in0=mask_rows[:]
+            .rearrange("p (b m) -> p b m", b=GRAPHS)
+            .unsqueeze(3)
+            .to_broadcast([P, GRAPHS, NODES, 2]),
+            scalar1=BF16_MAX,
+            scalar2=NEG_INF,
+            op0=ALU.mult,
+            op1=ALU.add,
+        )
+
+        x_grouped = {}
+        for b in range(GRAPHS):
+            x_grouped[b] = h_pool.tile([P, PACK, P, PACK], BF16, name="x_grouped", tag="h_grouped", align_bytes=64)
+            for half in range(2):
+                turn(x_rows[b][:, 2 * half : 2 * half + 2], x_grouped[b][:, 2 * half : 2 * half + 2])
+
+        def quantise_x(b):
+            nc.vector.quantize_mx(
+                out=x_codes[:, b, :].bitcast(FP8X4),
+                scales=x_planes[:, b, :],
+                in_=x_grouped[b][:].rearrange("q t n k -> q (t n k)"),
+            )
+
+        def live(i):
+            return 0 <= i < TILES
+
+        issued = 0
+        quantised = 0
+        for step in range(TILES + 4):
+            for j in range(PAIRS):
+                if live(step - 3) and j == 0:
+                    invert_sums(step - 3)
+                if live(step - 4) and j == 0:
+                    multiply(step - 4, 0)
+                    multiply(step - 4, 1)
+                if live(step):
+                    mask_scores(step, j)
+                for e in range(2):
+                    if live(step - 3):
+                        normalise(step - 3, 2 * j + e)
+                    if live(step - 4):
+                        add_relu(step - 4, 2 * j + e)
+                if live(step - 1):
+                    fold_maxima(step - 1, j)
+                if step == 0 and j == X_TICK:
+                    quantise_x(0)
+                    quantise_x(1)
+                quantised = quantise_h(quantised, issued)
+                if step > 0 or j > X_TICK:
+                    issued = project(issued, issued + H_BANKS_PER_TICK)
+                if live(step - 2):
+                    exponential(step - 2, 2 * j)
+                    exponential(step - 2, 2 * j + 1)
+                if live(step - 3):
+                    turn_att(step - 3, j)
+                if live(step - 4) and j + 1 < PAIRS:
+                    multiply(step - 4, 2 * j + 2)
+                    multiply(step - 4, 2 * j + 3)
+                if live(step - 3) and j >= 1:
+                    quantise_att(step - 3, j - 1)
+            if live(step - 3):
+                quantise_att(step - 3, PAIRS - 1)
+            if live(step - 4):
+                store(step - 4)
+            if live(step + 2):
+                load_scores(step + 2)

@@ -23,6 +23,7 @@ NODE_TILES = NODES // P
 TILES = GRAPHS * NODE_TILES
 NEG_INF = -1e30
 BF16_MAX = 3.3895313892515355e38
+MASK_PARTS = ((0, 2), (2, 5))
 FOLDS = 4
 H_BANKS = GRAPHS * RELS * (FEATS // P)
 H_BANKS_PER_TICK = 2
@@ -88,14 +89,15 @@ def tile_rgat_pa_e_kernel(tc, adj, x, dmask, W_words, W_scales, out):
                 in_=adj[b, t * P : (t + 1) * P].rearrange("n m r -> n (m r)"),
             )
 
-        def mask_scores(i, j):
+        def mask_scores(i, part):
             b = i // NODE_TILES
-            if j == 0:
+            if part == 0:
                 masked[i] = masked_pool.tile([P, PAIRS, NODES, 2], BF16, name="masked")
+            first, last = MASK_PARTS[part]
             nc.vector.tensor_tensor(
-                out=masked[i][:, j],
-                in0=scores[i][:].rearrange("p (m j e) -> p j m e", j=PAIRS, e=2)[:, j],
-                in1=ceiling[:, b],
+                out=masked[i][:, first:last].rearrange("p j m e -> p m j e"),
+                in0=scores[i][:].rearrange("p (m j e) -> p m j e", j=PAIRS, e=2)[:, :, first:last, :],
+                in1=ceiling[:, b].unsqueeze(2).to_broadcast([P, NODES, last - first, 2]),
                 op=ALU.min,
             )
 
@@ -289,7 +291,7 @@ def tile_rgat_pa_e_kernel(tc, adj, x, dmask, W_words, W_scales, out):
                 if live(step - 4) and j == 0:
                     multiply(step - 4, 0)
                     multiply(step - 4, 1)
-                if live(step):
+                if live(step) and j < len(MASK_PARTS):
                     mask_scores(step, j)
                 for e in range(2):
                     if live(step - 3):

@@ -28,6 +28,12 @@ FOLDS = 4
 H_BANKS = GRAPHS * RELS * (FEATS // P)
 H_BANKS_PER_TICK = 2
 X_TICK = 1
+FOLD_AT = len(MASK_PARTS) + 1
+EXP_AT = FOLD_AT + PAIRS + 1
+NORMALISE_AT = EXP_AT + PAIRS + 1
+QUANTISE_AT = NORMALISE_AT + 2
+MULTIPLY_AT = 4 * PAIRS
+ADD_AT = MULTIPLY_AT + 1
 
 FLOPS = 2 * 2 * GRAPHS * RELS * NODES * NODES * FEATS
 
@@ -215,19 +221,19 @@ def tile_rgat_pa_e_kernel(tc, adj, x, dmask, W_words, W_scales, out):
                 stop=True,
             )
 
+        def start_total(i):
+            total[i] = out_pool.tile([P, FEATS], F32, name="total")
+            nc.scalar.activation(out=total[i][:], in_=z_bank[(i, 0)][:], func=ACT.Relu)
+
         def add_relu(i, r):
-            if r == 0:
-                total[i] = out_pool.tile([P, FEATS], F32, name="total")
-                nc.scalar.activation(out=total[i][:], in_=z_bank[(i, r)][:], func=ACT.Relu)
-            else:
-                nc.vector.scalar_tensor_tensor(
-                    out=total[i][:],
-                    in0=z_bank[(i, r)][:],
-                    scalar=0.0,
-                    in1=total[i][:],
-                    op0=ALU.max,
-                    op1=ALU.add,
-                )
+            nc.vector.scalar_tensor_tensor(
+                out=total[i][:],
+                in0=z_bank[(i, r)][:],
+                scalar=0.0,
+                in1=total[i][:],
+                op0=ALU.max,
+                op1=ALU.add,
+            )
 
         def store(i):
             b, t = divmod(i, NODE_TILES)
@@ -250,8 +256,8 @@ def tile_rgat_pa_e_kernel(tc, adj, x, dmask, W_words, W_scales, out):
             )
         words_in_dram = W_words.rearrange("g p n t -> p g (n t)").bitcast(I32)
         nc.sync.dma_start(out=w_words[:, 0:2, :].bitcast(I32), in_=words_in_dram[:, 0:2, :])
-        nc.sync.dma_start(out=w_words[:, 2:5, :].bitcast(I32), in_=words_in_dram[:, 2:5, :])
         load_scores(1)
+        nc.sync.dma_start(out=w_words[:, 2:5, :].bitcast(I32), in_=words_in_dram[:, 2:5, :])
         nc.sync.dma_start(out=w_words[:, 5:10, :].bitcast(I32), in_=words_in_dram[:, 5:10, :])
 
         nc.vector.tensor_scalar(
@@ -279,46 +285,50 @@ def tile_rgat_pa_e_kernel(tc, adj, x, dmask, W_words, W_scales, out):
                 in_=x_grouped[b][:].rearrange("q t n k -> q (t n k)"),
             )
 
-        def live(i):
-            return 0 <= i < TILES
+        def due(tick, delay):
+            i, j = divmod(tick - delay, PAIRS)
+            return i, j, 0 <= i < TILES
 
         issued = 0
         quantised = 0
-        for step in range(TILES + 4):
-            for j in range(PAIRS):
-                if live(step - 3) and j == 0:
-                    invert_sums(step - 3)
-                if live(step - 4) and j == 0:
-                    multiply(step - 4, 0)
-                    multiply(step - 4, 1)
-                if live(step) and j < len(MASK_PARTS):
-                    mask_scores(step, j)
-                for e in range(2):
-                    if live(step - 3):
-                        normalise(step - 3, 2 * j + e)
-                    if live(step - 4):
-                        add_relu(step - 4, 2 * j + e)
-                if live(step - 1):
-                    fold_maxima(step - 1, j)
-                if step == 0 and j == X_TICK:
-                    quantise_x(0)
-                    quantise_x(1)
-                quantised = quantise_h(quantised, issued)
-                if step > 0 or j > X_TICK:
-                    issued = project(issued, issued + H_BANKS_PER_TICK)
-                if live(step - 2):
-                    exponential(step - 2, 2 * j)
-                    exponential(step - 2, 2 * j + 1)
-                if live(step - 3):
-                    turn_att(step - 3, j)
-                if live(step - 4) and j + 1 < PAIRS:
-                    multiply(step - 4, 2 * j + 2)
-                    multiply(step - 4, 2 * j + 3)
-                if live(step - 3) and j >= 1:
-                    quantise_att(step - 3, j - 1)
-            if live(step - 3):
-                quantise_att(step - 3, PAIRS - 1)
-            if live(step - 4):
-                store(step - 4)
-            if live(step + 2):
-                load_scores(step + 2)
+        for tick in range(TILES * PAIRS + ADD_AT):
+            i, j, live = due(tick, NORMALISE_AT)
+            i_add, j_add, adding = due(tick, ADD_AT)
+            if live and j == 0:
+                invert_sums(i)
+            for e in range(2):
+                if live:
+                    normalise(i, 2 * j + e)
+                if adding and 2 * j_add + e > 0:
+                    add_relu(i_add, 2 * j_add + e)
+            if adding and j_add == PAIRS - 1:
+                store(i_add)
+            if live:
+                turn_att(i, j)
+            i, j, live = due(tick, QUANTISE_AT)
+            if live:
+                quantise_att(i, j)
+            i, j, live = due(tick, MULTIPLY_AT)
+            if live:
+                multiply(i, 2 * j)
+                multiply(i, 2 * j + 1)
+                if j == 0:
+                    start_total(i)
+            i, j, live = due(tick, 0)
+            if live and j < len(MASK_PARTS):
+                mask_scores(i, j)
+            if live and j == len(MASK_PARTS) and i + 2 < TILES:
+                load_scores(i + 2)
+            i, j, live = due(tick, FOLD_AT)
+            if live:
+                fold_maxima(i, j)
+            if tick == X_TICK:
+                quantise_x(0)
+                quantise_x(1)
+            quantised = quantise_h(quantised, issued)
+            if tick > X_TICK:
+                issued = project(issued, issued + H_BANKS_PER_TICK)
+            i, j, live = due(tick, EXP_AT)
+            if live:
+                exponential(i, 2 * j)
+                exponential(i, 2 * j + 1)

@@ -31,7 +31,8 @@ X_TICK = 1
 FOLD_AT = len(MASK_PARTS) + 1
 EXP_AT = FOLD_AT + PAIRS + 1
 NORMALISE_AT = EXP_AT + PAIRS + 1
-QUANTISE_AT = NORMALISE_AT + 2
+TURN_AT = NORMALISE_AT + 1
+QUANTISE_AT = TURN_AT + 2
 MULTIPLY_AT = 4 * PAIRS
 ADD_AT = MULTIPLY_AT + 1
 
@@ -141,21 +142,25 @@ def tile_rgat_pa_e_kernel(tc, adj, x, dmask, W_words, W_scales, out):
                 accum_out=sums[i][:, r : r + 1],
             )
 
-        def invert_sums(i):
+        def invert_sums(i, j):
+            if j > 0:
+                nc.vector.reciprocal(out=inv_sum[i][:, 2 * j : 2 * j + 2], in_=sums[i][:, 2 * j : 2 * j + 2])
+                return
             inv_sum[i] = stat_pool.tile([P, RELS], F32, name="inv_sum")
-            nc.vector.reciprocal(out=inv_sum[i][:], in_=sums[i][:])
+            nc.vector.reciprocal(out=inv_sum[i][:, 0:2], in_=sums[i][:, 0:2])
             att_codes[i] = code_pool.tile([P, RELS, P], U32, name="att_codes", align_bytes=64)
             att_planes[i] = code_pool.tile([P, RELS, P], U8, name="att_planes", align_bytes=64)
 
         def normalise(i, r):
             if r % 2 == 0:
-                att[i] = att_pool.tile([P, 2, NODES], BF16, name="att")
-            nc.vector.tensor_scalar(
-                out=att[i][:, r % 2, :],
+                att[(i, r // 2)] = att_pool.tile([P, 2, NODES], BF16, name="att")
+            nc.gpsimd.tensor_scalar(
+                out=att[(i, r // 2)][:, r % 2, :],
                 in0=exps[i][:, r, :],
                 scalar1=inv_sum[i][:, r : r + 1],
-                scalar2=None,
+                scalar2=0.0,
                 op0=ALU.mult,
+                op1=ALU.add,
             )
 
         def turn(rows, grouped):
@@ -168,7 +173,7 @@ def tile_rgat_pa_e_kernel(tc, adj, x, dmask, W_words, W_scales, out):
 
         def turn_att(i, j):
             att_grouped[(i, j)] = att_pool.tile([P, 2, P, PACK], BF16, name="att_grouped", align_bytes=64)
-            turn(att[i][:], att_grouped[(i, j)][:])
+            turn(att[(i, j)][:], att_grouped[(i, j)][:])
 
         def quantise_att(i, j):
             nc.vector.quantize_mx(
@@ -294,8 +299,8 @@ def tile_rgat_pa_e_kernel(tc, adj, x, dmask, W_words, W_scales, out):
         for tick in range(TILES * PAIRS + ADD_AT):
             i, j, live = due(tick, NORMALISE_AT)
             i_add, j_add, adding = due(tick, ADD_AT)
-            if live and j == 0:
-                invert_sums(i)
+            if live:
+                invert_sums(i, j)
             for e in range(2):
                 if live:
                     normalise(i, 2 * j + e)
@@ -303,6 +308,7 @@ def tile_rgat_pa_e_kernel(tc, adj, x, dmask, W_words, W_scales, out):
                     add_relu(i_add, 2 * j_add + e)
             if adding and j_add == PAIRS - 1:
                 store(i_add)
+            i, j, live = due(tick, TURN_AT)
             if live:
                 turn_att(i, j)
             i, j, live = due(tick, QUANTISE_AT)

@@ -301,19 +301,21 @@ def tile_rgat_pa_e_kernel(tc, adj, x, dmask, W_words, W_scales, out):
             i_add, j_add, adding = due(tick, ADD_AT)
             if live:
                 invert_sums(i, j)
-            for e in range(2):
-                if live:
-                    normalise(i, 2 * j + e)
-                if adding and 2 * j_add + e > 0:
-                    add_relu(i_add, 2 * j_add + e)
+            if live:
+                normalise(i, 2 * j)
+                normalise(i, 2 * j + 1)
+            if adding and j_add > 0:
+                add_relu(i_add, 2 * j_add)
+            i, j, live = due(tick, QUANTISE_AT)
+            if live:
+                quantise_att(i, j)
+            if adding:
+                add_relu(i_add, 2 * j_add + 1)
             if adding and j_add == PAIRS - 1:
                 store(i_add)
             i, j, live = due(tick, TURN_AT)
             if live:
                 turn_att(i, j)
-            i, j, live = due(tick, QUANTISE_AT)
-            if live:
-                quantise_att(i, j)
             i, j, live = due(tick, MULTIPLY_AT)
             if live:
                 multiply(i, 2 * j)

@@ -31,8 +31,9 @@ X_TICK = 1
 FOLD_AT = len(MASK_PARTS) + 1
 EXP_AT = FOLD_AT + PAIRS + 1
 NORMALISE_AT = EXP_AT + PAIRS + 1
-TURN_AT = NORMALISE_AT + 1
-QUANTISE_AT = TURN_AT + 2
+TURN_AT = NORMALISE_AT + 2
+COPY_AT = TURN_AT + 1
+QUANTISE_AT = COPY_AT + 1
 MULTIPLY_AT = 4 * PAIRS
 ADD_AT = MULTIPLY_AT + 1
 
@@ -52,7 +53,7 @@ def tile_rgat_pa_e_kernel(tc, adj, x, dmask, W_words, W_scales, out):
         fold_pool = stack.enter_context(tc.tile_pool(name="fold_pool", bufs=1))
         stat_pool = stack.enter_context(tc.tile_pool(name="stat_pool", bufs=3))
         exp_pool = stack.enter_context(tc.tile_pool(name="exp_pool", bufs=2))
-        att_pool = stack.enter_context(tc.tile_pool(name="att_pool", bufs=3))
+        att_pool = stack.enter_context(tc.tile_pool(name="att_pool", bufs=4))
         code_pool = stack.enter_context(tc.tile_pool(name="code_pool", bufs=2))
         h_pool = stack.enter_context(tc.tile_pool(name="h_pool", bufs=2))
         out_pool = stack.enter_context(tc.tile_pool(name="out_pool", bufs=2))
@@ -81,6 +82,7 @@ def tile_rgat_pa_e_kernel(tc, adj, x, dmask, W_words, W_scales, out):
         sums = {}
         inv_sum = {}
         att = {}
+        att_turned = {}
         att_grouped = {}
         att_codes = {}
         att_planes = {}
@@ -142,12 +144,9 @@ def tile_rgat_pa_e_kernel(tc, adj, x, dmask, W_words, W_scales, out):
                 accum_out=sums[i][:, r : r + 1],
             )
 
-        def invert_sums(i, j):
-            if j > 0:
-                nc.vector.reciprocal(out=inv_sum[i][:, 2 * j : 2 * j + 2], in_=sums[i][:, 2 * j : 2 * j + 2])
-                return
+        def invert_sums(i):
             inv_sum[i] = stat_pool.tile([P, RELS], F32, name="inv_sum")
-            nc.vector.reciprocal(out=inv_sum[i][:, 0:2], in_=sums[i][:, 0:2])
+            nc.vector.reciprocal(out=inv_sum[i][:], in_=sums[i][:])
             att_codes[i] = code_pool.tile([P, RELS, P], U32, name="att_codes", align_bytes=64)
             att_planes[i] = code_pool.tile([P, RELS, P], U8, name="att_planes", align_bytes=64)
 
@@ -163,17 +162,23 @@ def tile_rgat_pa_e_kernel(tc, adj, x, dmask, W_words, W_scales, out):
                 op1=ALU.add,
             )
 
-        def turn(rows, grouped):
+        def turn(rows):
             rows_as_words = rows.bitcast(F32)
             turned = turned_banks.tile([P, 2, 2, P], F32, name="turned")
             for e in range(2):
                 for u in range(2):
                     nc.tensor.transpose(turned[:, e, u, :], rows_as_words[:, e, u : NODES // 2 : 2], ident[:])
+            return turned
+
+        def copy_turned(turned, grouped):
             nc.scalar.copy(out=grouped.bitcast(F32), in_=turned[:].rearrange("q e u n -> q e n u"))
 
         def turn_att(i, j):
+            att_turned[(i, j)] = turn(att[(i, j)][:])
+
+        def copy_att(i, j):
             att_grouped[(i, j)] = att_pool.tile([P, 2, P, PACK], BF16, name="att_grouped", align_bytes=64)
-            turn(att[(i, j)][:], att_grouped[(i, j)][:])
+            copy_turned(att_turned[(i, j)], att_grouped[(i, j)][:])
 
         def quantise_att(i, j):
             nc.vector.quantize_mx(
@@ -281,7 +286,7 @@ def tile_rgat_pa_e_kernel(tc, adj, x, dmask, W_words, W_scales, out):
         for b in range(GRAPHS):
             x_grouped[b] = h_pool.tile([P, PACK, P, PACK], BF16, name="x_grouped", tag="h_grouped", align_bytes=64)
             for half in range(2):
-                turn(x_rows[b][:, 2 * half : 2 * half + 2], x_grouped[b][:, 2 * half : 2 * half + 2])
+                copy_turned(turn(x_rows[b][:, 2 * half : 2 * half + 2]), x_grouped[b][:, 2 * half : 2 * half + 2])
 
         def quantise_x(b):
             nc.vector.quantize_mx(
@@ -299,8 +304,8 @@ def tile_rgat_pa_e_kernel(tc, adj, x, dmask, W_words, W_scales, out):
         for tick in range(TILES * PAIRS + ADD_AT):
             i, j, live = due(tick, NORMALISE_AT)
             i_add, j_add, adding = due(tick, ADD_AT)
-            if live:
-                invert_sums(i, j)
+            if live and j == 0:
+                invert_sums(i)
             if live:
                 normalise(i, 2 * j)
                 normalise(i, 2 * j + 1)
@@ -316,6 +321,9 @@ def tile_rgat_pa_e_kernel(tc, adj, x, dmask, W_words, W_scales, out):
             i, j, live = due(tick, TURN_AT)
             if live:
                 turn_att(i, j)
+            i, j, live = due(tick, COPY_AT)
+            if live:
+                copy_att(i, j)
             i, j, live = due(tick, MULTIPLY_AT)
             if live:
                 multiply(i, 2 * j)

@@ -52,7 +52,7 @@ def tile_rgat_pa_e_kernel(tc, adj, x, dmask, W_words, W_scales, out):
         masked_pool = stack.enter_context(tc.tile_pool(name="masked_pool", bufs=3))
         fold_pool = stack.enter_context(tc.tile_pool(name="fold_pool", bufs=1))
         stat_pool = stack.enter_context(tc.tile_pool(name="stat_pool", bufs=3))
-        exp_pool = stack.enter_context(tc.tile_pool(name="exp_pool", bufs=2))
+        exp_pool = stack.enter_context(tc.tile_pool(name="exp_pool", bufs=NORMALISE_AT - EXP_AT + 4))
         att_pool = stack.enter_context(tc.tile_pool(name="att_pool", bufs=4))
         code_pool = stack.enter_context(tc.tile_pool(name="code_pool", bufs=2))
         h_pool = stack.enter_context(tc.tile_pool(name="h_pool", bufs=2))
@@ -133,10 +133,11 @@ def tile_rgat_pa_e_kernel(tc, adj, x, dmask, W_words, W_scales, out):
 
         def exponential(i, r):
             if r == 0:
-                exps[i] = exp_pool.tile([P, RELS, NODES], F32, name="exps")
                 sums[i] = stat_pool.tile([P, RELS], F32, name="sums")
+            if r % 2 == 0:
+                exps[(i, r // 2)] = exp_pool.tile([P, 2, NODES], F32, name="exps")
             nc.scalar.activation(
-                out=exps[i][:, r, :],
+                out=exps[(i, r // 2)][:, r % 2, :],
                 in_=masked[i][:, r // 2, :, r % 2],
                 func=ACT.Exp,
                 bias=neg_max[i][:, r : r + 1],
@@ -155,7 +156,7 @@ def tile_rgat_pa_e_kernel(tc, adj, x, dmask, W_words, W_scales, out):
                 att[(i, r // 2)] = att_pool.tile([P, 2, NODES], BF16, name="att")
             nc.gpsimd.tensor_scalar(
                 out=att[(i, r // 2)][:, r % 2, :],
-                in0=exps[i][:, r, :],
+                in0=exps[(i, r // 2)][:, r % 2, :],
                 scalar1=inv_sum[i][:, r : r + 1],
                 scalar2=0.0,
                 op0=ALU.mult,
@@ -324,6 +325,9 @@ def tile_rgat_pa_e_kernel(tc, adj, x, dmask, W_words, W_scales, out):
             i, j, live = due(tick, COPY_AT)
             if live:
                 copy_att(i, j)
+            copied = issued
+            if tick > X_TICK:
+                issued = project(issued, issued + H_BANKS_PER_TICK)
             i, j, live = due(tick, MULTIPLY_AT)
             if live:
                 multiply(i, 2 * j)
@@ -341,9 +345,7 @@ def tile_rgat_pa_e_kernel(tc, adj, x, dmask, W_words, W_scales, out):
             if tick == X_TICK:
                 quantise_x(0)
                 quantise_x(1)
-            quantised = quantise_h(quantised, issued)
-            if tick > X_TICK:
-                issued = project(issued, issued + H_BANKS_PER_TICK)
+            quantised = quantise_h(quantised, copied)
             i, j, live = due(tick, EXP_AT)
             if live:
                 exponential(i, 2 * j)

@@ -26,7 +26,6 @@ BF16_MAX = 3.3895313892515355e38
 MASK_PARTS = ((0, 2), (2, 5))
 FOLDS = 4
 H_BANKS = GRAPHS * RELS * (FEATS // P)
-H_BANKS_PER_TICK = 2
 X_TICK = 1
 FOLD_AT = len(MASK_PARTS) + 1
 EXP_AT = FOLD_AT + PAIRS + 1
@@ -55,7 +54,7 @@ def tile_rgat_pa_e_kernel(tc, adj, x, dmask, W_words, W_scales, out):
         exp_pool = stack.enter_context(tc.tile_pool(name="exp_pool", bufs=NORMALISE_AT - EXP_AT + 4))
         att_pool = stack.enter_context(tc.tile_pool(name="att_pool", bufs=4))
         code_pool = stack.enter_context(tc.tile_pool(name="code_pool", bufs=2))
-        h_pool = stack.enter_context(tc.tile_pool(name="h_pool", bufs=2))
+        h_pool = stack.enter_context(tc.tile_pool(name="h_pool", bufs=3))
         out_pool = stack.enter_context(tc.tile_pool(name="out_pool", bufs=2))
 
         ident = keep.tile([P, P], F32, name="ident")
@@ -326,8 +325,12 @@ def tile_rgat_pa_e_kernel(tc, adj, x, dmask, W_words, W_scales, out):
             if live:
                 copy_att(i, j)
             copied = issued
-            if tick > X_TICK:
-                issued = project(issued, issued + H_BANKS_PER_TICK)
+            if X_TICK < tick < EXP_AT:
+                issued = project(issued, issued + 3)
+            elif EXP_AT <= tick < COPY_AT - 2:
+                issued = project(issued, issued + 1)
+            elif tick >= COPY_AT - 2:
+                issued = project(issued, issued + 2)
             i, j, live = due(tick, MULTIPLY_AT)
             if live:
                 multiply(i, 2 * j)

@@ -29,11 +29,11 @@ H_BANKS = GRAPHS * RELS * (FEATS // P)
 X_TICK = 1
 FOLD_AT = len(MASK_PARTS) + 1
 EXP_AT = FOLD_AT + PAIRS + 1
-NORMALISE_AT = EXP_AT + PAIRS + 1
-TURN_AT = NORMALISE_AT + 2
+NORMALISE_AT = EXP_AT + 2
+TURN_AT = NORMALISE_AT + 1
 COPY_AT = TURN_AT + 1
 QUANTISE_AT = COPY_AT + 1
-MULTIPLY_AT = 4 * PAIRS
+MULTIPLY_AT = QUANTISE_AT + 1
 ADD_AT = MULTIPLY_AT + 1
 
 FLOPS = 2 * 2 * GRAPHS * RELS * NODES * NODES * FEATS
@@ -144,11 +144,13 @@ def tile_rgat_pa_e_kernel(tc, adj, x, dmask, W_words, W_scales, out):
                 accum_out=sums[i][:, r : r + 1],
             )
 
-        def invert_sums(i):
-            inv_sum[i] = stat_pool.tile([P, RELS], F32, name="inv_sum")
-            nc.vector.reciprocal(out=inv_sum[i][:], in_=sums[i][:])
-            att_codes[i] = code_pool.tile([P, RELS, P], U32, name="att_codes", align_bytes=64)
-            att_planes[i] = code_pool.tile([P, RELS, P], U8, name="att_planes", align_bytes=64)
+        def invert_sums(i, j):
+            if j == 0:
+                inv_sum[i] = stat_pool.tile([P, RELS], F32, name="inv_sum")
+                att_codes[i] = code_pool.tile([P, RELS, P], U32, name="att_codes", align_bytes=64)
+                att_planes[i] = code_pool.tile([P, RELS, P], U8, name="att_planes", align_bytes=64)
+            pair = slice(2 * j, 2 * j + 2)
+            nc.vector.reciprocal(out=inv_sum[i][:, pair], in_=sums[i][:, pair])
 
         def normalise(i, r):
             if r % 2 == 0:
@@ -302,53 +304,50 @@ def tile_rgat_pa_e_kernel(tc, adj, x, dmask, W_words, W_scales, out):
         issued = 0
         quantised = 0
         for tick in range(TILES * PAIRS + ADD_AT):
-            i, j, live = due(tick, NORMALISE_AT)
             i_add, j_add, adding = due(tick, ADD_AT)
-            if live and j == 0:
-                invert_sums(i)
-            if live:
-                normalise(i, 2 * j)
-                normalise(i, 2 * j + 1)
             if adding and j_add > 0:
                 add_relu(i_add, 2 * j_add)
+            i, j, live = due(tick, FOLD_AT)
+            if live:
+                fold_maxima(i, j)
             i, j, live = due(tick, QUANTISE_AT)
             if live:
                 quantise_att(i, j)
-            if adding:
-                add_relu(i_add, 2 * j_add + 1)
-            if adding and j_add == PAIRS - 1:
-                store(i_add)
-            i, j, live = due(tick, TURN_AT)
-            if live:
-                turn_att(i, j)
-            i, j, live = due(tick, COPY_AT)
-            if live:
-                copy_att(i, j)
-            copied = issued
-            if X_TICK < tick < EXP_AT:
-                issued = project(issued, issued + 3)
-            elif EXP_AT <= tick < COPY_AT - 2:
-                issued = project(issued, issued + 1)
-            elif tick >= COPY_AT - 2:
-                issued = project(issued, issued + 2)
-            i, j, live = due(tick, MULTIPLY_AT)
-            if live:
-                multiply(i, 2 * j)
-                multiply(i, 2 * j + 1)
-                if j == 0:
-                    start_total(i)
             i, j, live = due(tick, 0)
             if live and j < len(MASK_PARTS):
                 mask_scores(i, j)
             if live and j == len(MASK_PARTS) and i + 2 < TILES:
                 load_scores(i + 2)
-            i, j, live = due(tick, FOLD_AT)
-            if live:
-                fold_maxima(i, j)
             if tick == X_TICK:
                 quantise_x(0)
                 quantise_x(1)
-            quantised = quantise_h(quantised, copied)
+            quantised = quantise_h(quantised, issued)
+            i, j, live = due(tick, NORMALISE_AT)
+            if live:
+                invert_sums(i, j)
+                normalise(i, 2 * j)
+                normalise(i, 2 * j + 1)
+            if adding:
+                add_relu(i_add, 2 * j_add + 1)
+            if adding and j_add == PAIRS - 1:
+                store(i_add)
+            i, j, live = due(tick, COPY_AT)
+            if live:
+                copy_att(i, j)
+            i, j, live = due(tick, MULTIPLY_AT)
+            if live:
+                multiply(i, 2 * j)
+                multiply(i, 2 * j + 1)
+            i_start, j_start, starting = i, j, live
+            if X_TICK < tick < EXP_AT:
+                issued = project(issued, issued + 3)
+            elif tick >= EXP_AT:
+                issued = project(issued, issued + 2)
+            i, j, live = due(tick, TURN_AT)
+            if live:
+                turn_att(i, j)
+            if starting and j_start == 0:
+                start_total(i_start)
             i, j, live = due(tick, EXP_AT)
             if live:
                 exponential(i, 2 * j)

@@ -305,14 +305,9 @@ def tile_rgat_pa_e_kernel(tc, adj, x, dmask, W_words, W_scales, out):
         quantised = 0
         for tick in range(TILES * PAIRS + ADD_AT):
             i_add, j_add, adding = due(tick, ADD_AT)
-            if adding and j_add > 0:
-                add_relu(i_add, 2 * j_add)
             i, j, live = due(tick, FOLD_AT)
             if live:
                 fold_maxima(i, j)
-            i, j, live = due(tick, QUANTISE_AT)
-            if live:
-                quantise_att(i, j)
             i, j, live = due(tick, 0)
             if live and j < len(MASK_PARTS):
                 mask_scores(i, j)
@@ -321,14 +316,19 @@ def tile_rgat_pa_e_kernel(tc, adj, x, dmask, W_words, W_scales, out):
             if tick == X_TICK:
                 quantise_x(0)
                 quantise_x(1)
-            quantised = quantise_h(quantised, issued)
             i, j, live = due(tick, NORMALISE_AT)
             if live:
                 invert_sums(i, j)
                 normalise(i, 2 * j)
                 normalise(i, 2 * j + 1)
+            if adding and j_add > 0:
+                add_relu(i_add, 2 * j_add)
+            i, j, live = due(tick, QUANTISE_AT)
+            if live:
+                quantise_att(i, j)
             if adding:
                 add_relu(i_add, 2 * j_add + 1)
+            quantised = quantise_h(quantised, issued)
             if adding and j_add == PAIRS - 1:
                 store(i_add)
             i, j, live = due(tick, COPY_AT)

@@ -26,7 +26,8 @@ BF16_MAX = 3.3895313892515355e38
 MASK_PARTS = ((0, 2), (2, 5))
 FOLDS = 4
 H_BANKS = GRAPHS * RELS * (FEATS // P)
-X_TICK = 1
+FIRST_H_TICK = 2
+X1_TICK = 12
 FOLD_AT = len(MASK_PARTS) + 1
 EXP_AT = FOLD_AT + PAIRS + 1
 NORMALISE_AT = EXP_AT + 2
@@ -256,21 +257,34 @@ def tile_rgat_pa_e_kernel(tc, adj, x, dmask, W_words, W_scales, out):
             out=mask_rows[:],
             in_=dmask.rearrange("b o m -> (b o m)").partition_broadcast(P),
         )
-        load_scores(0)
         x_rows = {}
         for b in range(GRAPHS):
             x_rows[b] = exp_pool.tile([P, PACK, FEATS], BF16, name="x_rows", tag="exps")
+
+        def load_x(b):
             nc.sync.dma_start(out=x_rows[b][:], in_=x[b].rearrange("(p t) f -> p t f", t=PACK))
-        for q in range(4):
-            nc.sync.dma_start(
-                out=w_planes[32 * q : 32 * q + 4].bitcast(I32),
-                in_=W_scales[:, 4 * q : 4 * q + 4, :].rearrange("g s n -> s g n").bitcast(I32),
-            )
+
         words_in_dram = W_words.rearrange("g p n t -> p g (n t)").bitcast(I32)
-        nc.sync.dma_start(out=w_words[:, 0:2, :].bitcast(I32), in_=words_in_dram[:, 0:2, :])
+
+        def load_w(first, last):
+            nc.sync.dma_start(out=w_words[:, first:last, :].bitcast(I32), in_=words_in_dram[:, first:last, :])
+
+        def load_w_scales():
+            for q in range(4):
+                nc.sync.dma_start(
+                    out=w_planes[32 * q : 32 * q + 4].bitcast(I32),
+                    in_=W_scales[:, 4 * q : 4 * q + 4, :].rearrange("g s n -> s g n").bitcast(I32),
+                )
+
+        load_x(0)
+        load_w_scales()
+        load_w(0, 2)
+        load_scores(0)
+        load_w(2, 4)
         load_scores(1)
-        nc.sync.dma_start(out=w_words[:, 2:5, :].bitcast(I32), in_=words_in_dram[:, 2:5, :])
-        nc.sync.dma_start(out=w_words[:, 5:10, :].bitcast(I32), in_=words_in_dram[:, 5:10, :])
+        load_x(1)
+        load_w(4, 7)
+        load_w(7, 10)
 
         nc.vector.tensor_scalar(
             out=ceiling[:],
@@ -285,7 +299,8 @@ def tile_rgat_pa_e_kernel(tc, adj, x, dmask, W_words, W_scales, out):
         )
 
         x_grouped = {}
-        for b in range(GRAPHS):
+
+        def turn_x(b):
             x_grouped[b] = h_pool.tile([P, PACK, P, PACK], BF16, name="x_grouped", tag="h_grouped", align_bytes=64)
             for half in range(2):
                 copy_turned(turn(x_rows[b][:, 2 * half : 2 * half + 2]), x_grouped[b][:, 2 * half : 2 * half + 2])
@@ -297,6 +312,9 @@ def tile_rgat_pa_e_kernel(tc, adj, x, dmask, W_words, W_scales, out):
                 in_=x_grouped[b][:].rearrange("q t n k -> q (t n k)"),
             )
 
+        turn_x(0)
+        quantise_x(0)
+
         def due(tick, delay):
             i, j = divmod(tick - delay, PAIRS)
             return i, j, 0 <= i < TILES
@@ -304,23 +322,18 @@ def tile_rgat_pa_e_kernel(tc, adj, x, dmask, W_words, W_scales, out):
         issued = 0
         quantised = 0
         for tick in range(TILES * PAIRS + ADD_AT):
-            i_add, j_add, adding = due(tick, ADD_AT)
-            i, j, live = due(tick, FOLD_AT)
-            if live:
-                fold_maxima(i, j)
-            i, j, live = due(tick, 0)
-            if live and j < len(MASK_PARTS):
-                mask_scores(i, j)
-            if live and j == len(MASK_PARTS) and i + 2 < TILES:
-                load_scores(i + 2)
-            if tick == X_TICK:
-                quantise_x(0)
-                quantise_x(1)
+            quantised = quantise_h(quantised, issued)
             i, j, live = due(tick, NORMALISE_AT)
             if live:
                 invert_sums(i, j)
                 normalise(i, 2 * j)
                 normalise(i, 2 * j + 1)
+            i, j, live = due(tick, FOLD_AT)
+            if live:
+                fold_maxima(i, j)
+            if tick == X1_TICK + 1:
+                quantise_x(1)
+            i_add, j_add, adding = due(tick, ADD_AT)
             if adding and j_add > 0:
                 add_relu(i_add, 2 * j_add)
             i, j, live = due(tick, QUANTISE_AT)
@@ -328,26 +341,32 @@ def tile_rgat_pa_e_kernel(tc, adj, x, dmask, W_words, W_scales, out):
                 quantise_att(i, j)
             if adding:
                 add_relu(i_add, 2 * j_add + 1)
-            quantised = quantise_h(quantised, issued)
             if adding and j_add == PAIRS - 1:
                 store(i_add)
+            i, j, live = due(tick, 0)
+            if live and j < len(MASK_PARTS):
+                mask_scores(i, j)
+            if live and j == len(MASK_PARTS) and i + 2 < TILES:
+                load_scores(i + 2)
             i, j, live = due(tick, COPY_AT)
             if live:
                 copy_att(i, j)
+            if tick == X1_TICK:
+                turn_x(1)
             i, j, live = due(tick, MULTIPLY_AT)
             if live:
                 multiply(i, 2 * j)
-                multiply(i, 2 * j + 1)
-            i_start, j_start, starting = i, j, live
-            if X_TICK < tick < EXP_AT:
+            if FIRST_H_TICK <= tick < EXP_AT:
                 issued = project(issued, issued + 3)
             elif tick >= EXP_AT:
                 issued = project(issued, issued + 2)
+            if live:
+                multiply(i, 2 * j + 1)
+                if j == 0:
+                    start_total(i)
             i, j, live = due(tick, TURN_AT)
             if live:
                 turn_att(i, j)
-            if starting and j_start == 0:
-                start_total(i_start)
             i, j, live = due(tick, EXP_AT)
             if live:
                 exponential(i, 2 * j)

@@ -27,9 +27,9 @@ MASK_PARTS = ((0, 2), (2, 5))
 FOLDS = 4
 H_BANKS = GRAPHS * RELS * (FEATS // P)
 FIRST_H_TICK = 2
-X1_TICK = 12
+X1_TICK = 6
 FOLD_AT = len(MASK_PARTS) + 1
-EXP_AT = FOLD_AT + PAIRS + 1
+EXP_AT = FOLD_AT + PAIRS + 2
 NORMALISE_AT = EXP_AT + 2
 TURN_AT = NORMALISE_AT + 1
 COPY_AT = TURN_AT + 1
@@ -55,13 +55,13 @@ def tile_rgat_pa_e_kernel(tc, adj, x, dmask, W_words, W_scales, out):
         exp_pool = stack.enter_context(tc.tile_pool(name="exp_pool", bufs=NORMALISE_AT - EXP_AT + 4))
         att_pool = stack.enter_context(tc.tile_pool(name="att_pool", bufs=4))
         code_pool = stack.enter_context(tc.tile_pool(name="code_pool", bufs=2))
-        h_pool = stack.enter_context(tc.tile_pool(name="h_pool", bufs=3))
+        h_pool = stack.enter_context(tc.tile_pool(name="h_pool", bufs=4))
         out_pool = stack.enter_context(tc.tile_pool(name="out_pool", bufs=2))
 
         ident = keep.tile([P, P], F32, name="ident")
-        make_identity(nc, ident[:])
 
-        mask_rows = keep.tile([P, GRAPHS * NODES], BF16, name="mask_rows")
+        mask_stage = keep.tile([P, GRAPHS * NODES], BF16, name="mask_stage")
+        ones = keep.tile([P, P], BF16, name="ones")
         ceiling = keep.tile([P, GRAPHS, NODES, 2], BF16, name="ceiling")
         w_words = keep.tile([P, RELS, FEATS], U32, name="w_words", align_bytes=64)
         w_planes = keep.tile([P, RELS, FEATS], U8, name="w_planes", align_bytes=64)
@@ -153,10 +153,13 @@ def tile_rgat_pa_e_kernel(tc, adj, x, dmask, W_words, W_scales, out):
             pair = slice(2 * j, 2 * j + 2)
             nc.vector.reciprocal(out=inv_sum[i][:, pair], in_=sums[i][:, pair])
 
-        def normalise(i, r):
+        def on_vector(i, j):
+            return i >= TILES - 2 and j in (1, 3)
+
+        def normalise(engine, i, r):
             if r % 2 == 0:
                 att[(i, r // 2)] = att_pool.tile([P, 2, NODES], BF16, name="att")
-            nc.gpsimd.tensor_scalar(
+            engine.tensor_scalar(
                 out=att[(i, r // 2)][:, r % 2, :],
                 in0=exps[(i, r // 2)][:, r % 2, :],
                 scalar1=inv_sum[i][:, r : r + 1],
@@ -208,8 +211,17 @@ def tile_rgat_pa_e_kernel(tc, adj, x, dmask, W_words, W_scales, out):
                         start=True,
                         stop=True,
                     )
-                nc.scalar.copy(out=h_grouped[(b, r)][:, cols, :], in_=h_bank[:].rearrange("p t w -> p w t"))
+                bank_by_columns = h_bank[:].rearrange("p t w -> p w t")
+                if 24 <= k < 40 and k % 4 == 0:
+                    late.append((h_grouped[(b, r)][:, cols, :], bank_by_columns))
+                else:
+                    nc.scalar.copy(out=h_grouped[(b, r)][:, cols, :], in_=bank_by_columns)
             return min(last_bank, H_BANKS)
+
+        def copy_late():
+            for grouped, bank_by_columns in late:
+                nc.vector.tensor_copy(out=grouped, in_=bank_by_columns)
+            late.clear()
 
         def quantise_h(first_bank, last_bank):
             for unit in range(first_bank // 4, last_bank // 4):
@@ -253,10 +265,10 @@ def tile_rgat_pa_e_kernel(tc, adj, x, dmask, W_words, W_scales, out):
             nc.sync.dma_start(out=out[b, t * P : (t + 1) * P, :], in_=total[i][:])
 
         nc.vector.memset(w_planes[:].bitcast(I32), 0)
-        nc.scalar.dma_start(
-            out=mask_rows[:],
-            in_=dmask.rearrange("b o m -> (b o m)").partition_broadcast(P),
-        )
+        nc.gpsimd.memset(mask_stage[:].bitcast(I32), 0)
+        nc.scalar.dma_start(out=mask_stage[0:1, :], in_=dmask.rearrange("b o m -> o (b m)"))
+        nc.gpsimd.memset(ones[:], 1.0)
+        make_identity(nc, ident[:])
         x_rows = {}
         for b in range(GRAPHS):
             x_rows[b] = exp_pool.tile([P, PACK, FEATS], BF16, name="x_rows", tag="exps")
@@ -286,19 +298,26 @@ def tile_rgat_pa_e_kernel(tc, adj, x, dmask, W_words, W_scales, out):
         load_w(4, 7)
         load_w(7, 10)
 
-        nc.vector.tensor_scalar(
-            out=ceiling[:],
-            in0=mask_rows[:]
-            .rearrange("p (b m) -> p b m", b=GRAPHS)
-            .unsqueeze(3)
-            .to_broadcast([P, GRAPHS, NODES, 2]),
-            scalar1=BF16_MAX,
-            scalar2=NEG_INF,
-            op0=ALU.mult,
-            op1=ALU.add,
-        )
+        for b in range(GRAPHS):
+            mask_bank = h_banks.tile([P, NODES], F32, name="mask_bank", tag="h_bank")
+            nc.tensor.matmul(
+                out=mask_bank[:],
+                lhsT=ones[:],
+                rhs=mask_stage[:, b * NODES : (b + 1) * NODES],
+                start=True,
+                stop=True,
+            )
+            nc.vector.tensor_scalar(
+                out=ceiling[:, b],
+                in0=mask_bank[:].unsqueeze(2).to_broadcast([P, NODES, 2]),
+                scalar1=BF16_MAX,
+                scalar2=NEG_INF,
+                op0=ALU.mult,
+                op1=ALU.add,
+            )
 
         x_grouped = {}
+        late = []
 
         def turn_x(b):
             x_grouped[b] = h_pool.tile([P, PACK, P, PACK], BF16, name="x_grouped", tag="h_grouped", align_bytes=64)
@@ -322,51 +341,56 @@ def tile_rgat_pa_e_kernel(tc, adj, x, dmask, W_words, W_scales, out):
         issued = 0
         quantised = 0
         for tick in range(TILES * PAIRS + ADD_AT):
-            quantised = quantise_h(quantised, issued)
             i, j, live = due(tick, NORMALISE_AT)
             if live:
                 invert_sums(i, j)
-                normalise(i, 2 * j)
-                normalise(i, 2 * j + 1)
-            i, j, live = due(tick, FOLD_AT)
+                normalise(nc.gpsimd, i, 2 * j)
+                if not on_vector(i, j):
+                    normalise(nc.gpsimd, i, 2 * j + 1)
+            i, j, live = due(tick, COPY_AT)
             if live:
-                fold_maxima(i, j)
-            if tick == X1_TICK + 1:
-                quantise_x(1)
+                copy_att(i, j)
+            if tick == X1_TICK:
+                turn_x(1)
+            banks = 0 if tick < FIRST_H_TICK else 3 if tick < EXP_AT else 2
+            issued = project(issued, issued + max(banks - 1, 0))
             i_add, j_add, adding = due(tick, ADD_AT)
             if adding and j_add > 0:
                 add_relu(i_add, 2 * j_add)
             i, j, live = due(tick, QUANTISE_AT)
             if live:
                 quantise_att(i, j)
+            copy_late()
+            if tick == X1_TICK + 1:
+                quantise_x(1)
             if adding:
                 add_relu(i_add, 2 * j_add + 1)
             if adding and j_add == PAIRS - 1:
                 store(i_add)
+            i, j, live = due(tick, NORMALISE_AT)
+            if live and on_vector(i, j):
+                normalise(nc.vector, i, 2 * j + 1)
             i, j, live = due(tick, 0)
             if live and j < len(MASK_PARTS):
                 mask_scores(i, j)
             if live and j == len(MASK_PARTS) and i + 2 < TILES:
                 load_scores(i + 2)
-            i, j, live = due(tick, COPY_AT)
+            i, j, live = due(tick, FOLD_AT)
             if live:
-                copy_att(i, j)
-            if tick == X1_TICK:
-                turn_x(1)
+                fold_maxima(i, j)
             i, j, live = due(tick, MULTIPLY_AT)
             if live:
                 multiply(i, 2 * j)
-            if FIRST_H_TICK <= tick < EXP_AT:
-                issued = project(issued, issued + 3)
-            elif tick >= EXP_AT:
-                issued = project(issued, issued + 2)
-            if live:
-                multiply(i, 2 * j + 1)
                 if j == 0:
                     start_total(i)
+            quantised = quantise_h(quantised, issued)
+            issued = project(issued, issued + min(banks, 1))
             i, j, live = due(tick, TURN_AT)
             if live:
                 turn_att(i, j)
+            i, j, live = due(tick, MULTIPLY_AT)
+            if live:
+                multiply(i, 2 * j + 1)
             i, j, live = due(tick, EXP_AT)
             if live:
                 exponential(i, 2 * j)

@@ -211,17 +211,8 @@ def tile_rgat_pa_e_kernel(tc, adj, x, dmask, W_words, W_scales, out):
                         start=True,
                         stop=True,
                     )
-                bank_by_columns = h_bank[:].rearrange("p t w -> p w t")
-                if 24 <= k < 40 and k % 4 == 0:
-                    late.append((h_grouped[(b, r)][:, cols, :], bank_by_columns))
-                else:
-                    nc.scalar.copy(out=h_grouped[(b, r)][:, cols, :], in_=bank_by_columns)
+                nc.scalar.copy(out=h_grouped[(b, r)][:, cols, :], in_=h_bank[:].rearrange("p t w -> p w t"))
             return min(last_bank, H_BANKS)
-
-        def copy_late():
-            for grouped, bank_by_columns in late:
-                nc.vector.tensor_copy(out=grouped, in_=bank_by_columns)
-            late.clear()
 
         def quantise_h(first_bank, last_bank):
             for unit in range(first_bank // 4, last_bank // 4):
@@ -317,7 +308,6 @@ def tile_rgat_pa_e_kernel(tc, adj, x, dmask, W_words, W_scales, out):
             )
 
         x_grouped = {}
-        late = []
 
         def turn_x(b):
             x_grouped[b] = h_pool.tile([P, PACK, P, PACK], BF16, name="x_grouped", tag="h_grouped", align_bytes=64)
@@ -360,7 +350,6 @@ def tile_rgat_pa_e_kernel(tc, adj, x, dmask, W_words, W_scales, out):
             i, j, live = due(tick, QUANTISE_AT)
             if live:
                 quantise_att(i, j)
-            copy_late()
             if tick == X1_TICK + 1:
                 quantise_x(1)
             if adding:

@@ -224,9 +224,14 @@ def tile_rgat_pa_e_kernel(tc, adj, x, dmask, W_words, W_scales, out):
                 )
             return last_bank
 
+        issued = 0
+
         def multiply(i, r):
             b = i // NODE_TILES
-            z_bank[(i, r)] = z_banks.tile([P, FEATS], F32, name="z_bank")
+            if issued == H_BANKS and r % 2 == 1:
+                z_bank[(i, r)] = h_banks.tile([P, FEATS], F32, name="z_bank", tag="h_bank")
+            else:
+                z_bank[(i, r)] = z_banks.tile([P, FEATS], F32, name="z_bank")
             nc.tensor.matmul_mx(
                 out=z_bank[(i, r)][:],
                 lhsT=att_codes[i][:, r, :].bitcast(FP8X4),
@@ -257,7 +262,6 @@ def tile_rgat_pa_e_kernel(tc, adj, x, dmask, W_words, W_scales, out):
 
         nc.vector.memset(w_planes[:].bitcast(I32), 0)
         nc.gpsimd.memset(mask_stage[:].bitcast(I32), 0)
-        nc.scalar.dma_start(out=mask_stage[0:1, :], in_=dmask.rearrange("b o m -> o (b m)"))
         nc.gpsimd.memset(ones[:], 1.0)
         make_identity(nc, ident[:])
         x_rows = {}
@@ -280,9 +284,10 @@ def tile_rgat_pa_e_kernel(tc, adj, x, dmask, W_words, W_scales, out):
                 )
 
         load_x(0)
+        nc.sync.dma_start(out=mask_stage[0:1, :], in_=dmask.rearrange("b o m -> o (b m)"))
+        load_scores(0)
         load_w_scales()
         load_w(0, 2)
-        load_scores(0)
         load_w(2, 4)
         load_scores(1)
         load_x(1)
@@ -328,7 +333,6 @@ def tile_rgat_pa_e_kernel(tc, adj, x, dmask, W_words, W_scales, out):
             i, j = divmod(tick - delay, PAIRS)
             return i, j, 0 <= i < TILES
 
-        issued = 0
         quantised = 0
         for tick in range(TILES * PAIRS + ADD_AT):
             i, j, live = due(tick, NORMALISE_AT)
@@ -345,15 +349,15 @@ def tile_rgat_pa_e_kernel(tc, adj, x, dmask, W_words, W_scales, out):
             banks = 0 if tick < FIRST_H_TICK else 3 if tick < EXP_AT else 2
             issued = project(issued, issued + max(banks - 1, 0))
             i_add, j_add, adding = due(tick, ADD_AT)
-            if adding and j_add > 0:
-                add_relu(i_add, 2 * j_add)
+            if adding:
+                add_relu(i_add, 2 * j_add + 1)
             i, j, live = due(tick, QUANTISE_AT)
             if live:
                 quantise_att(i, j)
             if tick == X1_TICK + 1:
                 quantise_x(1)
-            if adding:
-                add_relu(i_add, 2 * j_add + 1)
+            if adding and j_add > 0:
+                add_relu(i_add, 2 * j_add)
             if adding and j_add == PAIRS - 1:
                 store(i_add)
             i, j, live = due(tick, NORMALISE_AT)
@@ -370,6 +374,7 @@ def tile_rgat_pa_e_kernel(tc, adj, x, dmask, W_words, W_scales, out):
             i, j, live = due(tick, MULTIPLY_AT)
             if live:
                 multiply(i, 2 * j)
+                multiply(i, 2 * j + 1)
                 if j == 0:
                     start_total(i)
             quantised = quantise_h(quantised, issued)
@@ -377,9 +382,6 @@ def tile_rgat_pa_e_kernel(tc, adj, x, dmask, W_words, W_scales, out):
             i, j, live = due(tick, TURN_AT)
             if live:
                 turn_att(i, j)
-            i, j, live = due(tick, MULTIPLY_AT)
-            if live:
-                multiply(i, 2 * j + 1)
             i, j, live = due(tick, EXP_AT)
             if live:
                 exponential(i, 2 * j)

from contextlib import ExitStack

import concourse.mybir as mybir
from concourse.masks import make_identity

F32 = mybir.dt.float32
BF16 = mybir.dt.bfloat16
I32 = mybir.dt.int32
U32 = mybir.dt.uint32
U8 = mybir.dt.uint8
FP8X4 = mybir.dt.float8_e4m3fn_x4
ALU = mybir.AluOpType
ACT = mybir.ActivationFunctionType

P = 128
PACK = 4
GRAPHS = 2
NODES = 512
FEATS = 512
RELS = 10
PAIRS = RELS // 2
NODE_TILES = NODES // P
TILES = GRAPHS * NODE_TILES
NEG_INF = -1e30
BF16_MAX = 3.3895313892515355e38
MASK_PARTS = ((0, 2), (2, 5))
FOLDS = 4
H_BANKS = GRAPHS * RELS * (FEATS // P)
FIRST_H_TICK = 2
X1_TICK = 6
FOLD_AT = len(MASK_PARTS) + 1
EXP_AT = FOLD_AT + PAIRS + 2
NORMALISE_AT = EXP_AT + 2
TURN_AT = NORMALISE_AT + 1
COPY_AT = TURN_AT + 1
QUANTISE_AT = COPY_AT + 1
MULTIPLY_AT = QUANTISE_AT + 1
ADD_AT = MULTIPLY_AT + 1

FLOPS = 2 * 2 * GRAPHS * RELS * NODES * NODES * FEATS


def tile_rgat_pa_e_kernel(tc, adj, x, dmask, W_words, W_scales, out):
    nc = tc.nc
    with ExitStack() as stack:
        stack.enter_context(tc.manual_schedule())
        keep = stack.enter_context(tc.tile_pool(name="keep", bufs=1))
        turned_banks = stack.enter_context(tc.psum_pool(name="turned_banks", bufs=2))
        h_banks = stack.enter_context(tc.psum_pool(name="h_banks", bufs=3))
        z_banks = stack.enter_context(tc.psum_pool(name="z_banks", bufs=3))
        score_pool = stack.enter_context(tc.tile_pool(name="score_pool", bufs=2))
        masked_pool = stack.enter_context(tc.tile_pool(name="masked_pool", bufs=3))
        fold_pool = stack.enter_context(tc.tile_pool(name="fold_pool", bufs=1))
        stat_pool = stack.enter_context(tc.tile_pool(name="stat_pool", bufs=3))
        exp_pool = stack.enter_context(tc.tile_pool(name="exp_pool", bufs=NORMALISE_AT - EXP_AT + 4))
        att_pool = stack.enter_context(tc.tile_pool(name="att_pool", bufs=4))
        code_pool = stack.enter_context(tc.tile_pool(name="code_pool", bufs=2))
        h_pool = stack.enter_context(tc.tile_pool(name="h_pool", bufs=4))
        out_pool = stack.enter_context(tc.tile_pool(name="out_pool", bufs=2))

        ident = keep.tile([P, P], F32, name="ident")

        mask_stage = keep.tile([P, GRAPHS * NODES], BF16, name="mask_stage")
        ones = keep.tile([P, P], BF16, name="ones")
        ceiling = keep.tile([P, GRAPHS, NODES, 2], BF16, name="ceiling")
        w_words = keep.tile([P, RELS, FEATS], U32, name="w_words", align_bytes=64)
        w_planes = keep.tile([P, RELS, FEATS], U8, name="w_planes", align_bytes=64)
        x_codes = keep.tile([P, GRAPHS, NODES], U32, name="x_codes", align_bytes=64)
        x_planes = keep.tile([P, GRAPHS, NODES], U8, name="x_planes", align_bytes=64)
        h_codes = {}
        h_planes = {}
        for b in range(GRAPHS):
            for r in range(RELS):
                h_codes[(b, r)] = keep.tile([P, FEATS], U32, name="h_codes_%d_%d" % (b, r), align_bytes=64)
                h_planes[(b, r)] = keep.tile([P, FEATS], U8, name="h_planes_%d_%d" % (b, r), align_bytes=64)

        scores = {}
        masked = {}
        folded = {}
        neg_max = {}
        exps = {}
        sums = {}
        inv_sum = {}
        att = {}
        att_turned = {}
        att_grouped = {}
        att_codes = {}
        att_planes = {}
        h_grouped = {}
        z_bank = {}
        total = {}

        def load_scores(i):
            b, t = divmod(i, NODE_TILES)
            scores[i] = score_pool.tile([P, NODES * RELS], BF16, name="scores")
            nc.sync.dma_start(
                out=scores[i][:],
                in_=adj[b, t * P : (t + 1) * P].rearrange("n m r -> n (m r)"),
            )

        def mask_scores(i, part):
            b = i // NODE_TILES
            if part == 0:
                masked[i] = masked_pool.tile([P, PAIRS, NODES, 2], BF16, name="masked")
            first, last = MASK_PARTS[part]
            nc.vector.tensor_tensor(
                out=masked[i][:, first:last].rearrange("p j m e -> p m j e"),
                in0=scores[i][:].rearrange("p (m j e) -> p m j e", j=PAIRS, e=2)[:, :, first:last, :],
                in1=ceiling[:, b].unsqueeze(2).to_broadcast([P, NODES, last - first, 2]),
                op=ALU.min,
            )

        def fold_maxima(i, depth):
            if depth < FOLDS:
                wide = masked[i][:].rearrange("p j m e -> p j (m e)") if depth == 0 else folded[i][:]
                width = NODES >> depth
                folded[i] = fold_pool.tile([P, PAIRS, width], BF16, name="folded_%d" % depth)
                nc.vector.tensor_tensor(
                    out=folded[i][:],
                    in0=wide[:, :, 0:width],
                    in1=wide[:, :, width : 2 * width],
                    op=ALU.max,
                )
            else:
                neg_max[i] = stat_pool.tile([P, RELS], F32, name="neg_max")
                nc.vector.tensor_reduce(
                    out=neg_max[i][:].rearrange("p (j e) -> p j e", e=2),
                    in_=folded[i][:].rearrange("p j (m e) -> p j e m", e=2),
                    axis=mybir.AxisListType.X,
                    op=ALU.max,
                    negate=True,
                )

        def exponential(i, r):
            if r == 0:
                sums[i] = stat_pool.tile([P, RELS], F32, name="sums")
            if r % 2 == 0:
                exps[(i, r // 2)] = exp_pool.tile([P, 2, NODES], F32, name="exps")
            nc.scalar.activation(
                out=exps[(i, r // 2)][:, r % 2, :],
                in_=masked[i][:, r // 2, :, r % 2],
                func=ACT.Exp,
                bias=neg_max[i][:, r : r + 1],
                scale=1.0,
                accum_out=sums[i][:, r : r + 1],
            )

        def invert_sums(i, j):
            if j == 0:
                inv_sum[i] = stat_pool.tile([P, RELS], F32, name="inv_sum")
                att_codes[i] = code_pool.tile([P, RELS, P], U32, name="att_codes", align_bytes=64)
                att_planes[i] = code_pool.tile([P, RELS, P], U8, name="att_planes", align_bytes=64)
            pair = slice(2 * j, 2 * j + 2)
            nc.vector.reciprocal(out=inv_sum[i][:, pair], in_=sums[i][:, pair])

        def on_vector(i, j):
            return i >= TILES - 2 and j in (1, 3)

        def normalise(engine, i, r):
            if r % 2 == 0:
                att[(i, r // 2)] = att_pool.tile([P, 2, NODES], BF16, name="att")
            engine.tensor_scalar(
                out=att[(i, r // 2)][:, r % 2, :],
                in0=exps[(i, r // 2)][:, r % 2, :],
                scalar1=inv_sum[i][:, r : r + 1],
                scalar2=0.0,
                op0=ALU.mult,
                op1=ALU.add,
            )

        def turn(rows):
            rows_as_words = rows.bitcast(F32)
            turned = turned_banks.tile([P, 2, 2, P], F32, name="turned")
            for e in range(2):
                for u in range(2):
                    nc.tensor.transpose(turned[:, e, u, :], rows_as_words[:, e, u : NODES // 2 : 2], ident[:])
            return turned

        def copy_turned(turned, grouped):
            nc.scalar.copy(out=grouped.bitcast(F32), in_=turned[:].rearrange("q e u n -> q e n u"))

        def turn_att(i, j):
            att_turned[(i, j)] = turn(att[(i, j)][:])

        def copy_att(i, j):
            att_grouped[(i, j)] = att_pool.tile([P, 2, P, PACK], BF16, name="att_grouped", align_bytes=64)
            copy_turned(att_turned[(i, j)], att_grouped[(i, j)][:])

        def quantise_att(i, j):
            nc.vector.quantize_mx(
                out=att_codes[i][:, 2 * j : 2 * j + 2, :].rearrange("q e n -> q (e n)").bitcast(FP8X4),
                scales=att_planes[i][:, 2 * j : 2 * j + 2, :].rearrange("q e n -> q (e n)"),
                in_=att_grouped[(i, j)][:].rearrange("q e n k -> q (e n k)"),
            )

        def project(first_bank, last_bank):
            for k in range(first_bank, min(last_bank, H_BANKS)):
                b, r, c = k // (4 * RELS), (k // 4) % RELS, k % 4
                if c == 0:
                    h_grouped[(b, r)] = h_pool.tile([P, FEATS, PACK], BF16, name="h_grouped", align_bytes=64)
                cols = slice(c * P, (c + 1) * P)
                h_bank = h_banks.tile([P, PACK, P], F32, name="h_bank")
                for t in range(PACK):
                    nodes = slice(t * P, (t + 1) * P)
                    nc.tensor.matmul_mx(
                        out=h_bank[:, t, :],
                        lhsT=x_codes[:, b, nodes].bitcast(FP8X4),
                        lhsT_scale=x_planes[:, b, nodes],
                        rhs=w_words[:, r, cols].bitcast(FP8X4),
                        rhs_scale=w_planes[:, r, cols],
                        start=True,
                        stop=True,
                    )
                nc.scalar.copy(out=h_grouped[(b, r)][:, cols, :], in_=h_bank[:].rearrange("p t w -> p w t"))
            return min(last_bank, H_BANKS)

        def quantise_h(first_bank, last_bank):
            for unit in range(first_bank // 4, last_bank // 4):
                b, r = divmod(unit, RELS)
                nc.vector.quantize_mx(
                    out=h_codes[(b, r)][:].bitcast(FP8X4),
                    scales=h_planes[(b, r)][:],
                    in_=h_grouped[(b, r)][:].rearrange("p w t -> p (w t)"),
                )
            return last_bank

        issued = 0

        def multiply(i, r):
            b = i // NODE_TILES
            if issued == H_BANKS and r % 2 == 1:
                z_bank[(i, r)] = h_banks.tile([P, FEATS], F32, name="z_bank", tag="h_bank")
            else:
                z_bank[(i, r)] = z_banks.tile([P, FEATS], F32, name="z_bank")
            nc.tensor.matmul_mx(
                out=z_bank[(i, r)][:],
                lhsT=att_codes[i][:, r, :].bitcast(FP8X4),
                lhsT_scale=att_planes[i][:, r, :],
                rhs=h_codes[(b, r)][:].bitcast(FP8X4),
                rhs_scale=h_planes[(b, r)][:],
                start=True,
                stop=True,
            )

        def start_total(i):
            total[i] = out_pool.tile([P, FEATS], F32, name="total")
            nc.scalar.activation(out=total[i][:], in_=z_bank[(i, 0)][:], func=ACT.Relu)

        def add_relu(i, r):
            nc.vector.scalar_tensor_tensor(
                out=total[i][:],
                in0=z_bank[(i, r)][:],
                scalar=0.0,
                in1=total[i][:],
                op0=ALU.max,
                op1=ALU.add,
            )

        def store(i):
            b, t = divmod(i, NODE_TILES)
            nc.sync.dma_start(out=out[b, t * P : (t + 1) * P, :], in_=total[i][:])

        nc.vector.memset(w_planes[:].bitcast(I32), 0)
        nc.gpsimd.memset(mask_stage[:].bitcast(I32), 0)
        nc.gpsimd.memset(ones[:], 1.0)
        make_identity(nc, ident[:])
        x_rows = {}
        for b in range(GRAPHS):
            x_rows[b] = exp_pool.tile([P, PACK, FEATS], BF16, name="x_rows", tag="exps")

        def load_x(b):
            nc.sync.dma_start(out=x_rows[b][:], in_=x[b].rearrange("(p t) f -> p t f", t=PACK))

        words_in_dram = W_words.rearrange("g p n t -> p g (n t)").bitcast(I32)

        def load_w(first, last):
            nc.sync.dma_start(out=w_words[:, first:last, :].bitcast(I32), in_=words_in_dram[:, first:last, :])

        def load_w_scales():
            for q in range(4):
                nc.sync.dma_start(
                    out=w_planes[32 * q : 32 * q + 4].bitcast(I32),
                    in_=W_scales[:, 4 * q : 4 * q + 4, :].rearrange("g s n -> s g n").bitcast(I32),
                )

        load_x(0)
        nc.sync.dma_start(out=mask_stage[0:1, :], in_=dmask.rearrange("b o m -> o (b m)"))
        load_scores(0)
        load_w_scales()
        load_w(0, 2)
        load_w(2, 4)
        load_scores(1)
        load_x(1)
        load_w(4, 7)
        load_w(7, 10)

        for b in range(GRAPHS):
            mask_bank = h_banks.tile([P, NODES], F32, name="mask_bank", tag="h_bank")
            nc.tensor.matmul(
                out=mask_bank[:],
                lhsT=ones[:],
                rhs=mask_stage[:, b * NODES : (b + 1) * NODES],
                start=True,
                stop=True,
            )
            nc.vector.tensor_scalar(
                out=ceiling[:, b],
                in0=mask_bank[:].unsqueeze(2).to_broadcast([P, NODES, 2]),
                scalar1=BF16_MAX,
                scalar2=NEG_INF,
                op0=ALU.mult,
                op1=ALU.add,
            )

        x_grouped = {}

        def turn_x(b):
            x_grouped[b] = h_pool.tile([P, PACK, P, PACK], BF16, name="x_grouped", tag="h_grouped", align_bytes=64)
            for half in range(2):
                copy_turned(turn(x_rows[b][:, 2 * half : 2 * half + 2]), x_grouped[b][:, 2 * half : 2 * half + 2])

        def quantise_x(b):
            nc.vector.quantize_mx(
                out=x_codes[:, b, :].bitcast(FP8X4),
                scales=x_planes[:, b, :],
                in_=x_grouped[b][:].rearrange("q t n k -> q (t n k)"),
            )

        turn_x(0)
        quantise_x(0)

        def due(tick, delay):
            i, j = divmod(tick - delay, PAIRS)
            return i, j, 0 <= i < TILES

        quantised = 0
        for tick in range(TILES * PAIRS + ADD_AT):
            i, j, live = due(tick, NORMALISE_AT)
            if live:
                invert_sums(i, j)
                normalise(nc.gpsimd, i, 2 * j)
                if not on_vector(i, j):
                    normalise(nc.gpsimd, i, 2 * j + 1)
            i, j, live = due(tick, COPY_AT)
            if live:
                copy_att(i, j)
            if tick == X1_TICK:
                turn_x(1)
            banks = 0 if tick < FIRST_H_TICK else 3 if tick < EXP_AT else 2
            issued = project(issued, issued + max(banks - 1, 0))
            i_add, j_add, adding = due(tick, ADD_AT)
            if adding:
                add_relu(i_add, 2 * j_add + 1)
            i, j, live = due(tick, QUANTISE_AT)
            if live:
                quantise_att(i, j)
            if tick == X1_TICK + 1:
                quantise_x(1)
            if adding and j_add > 0:
                add_relu(i_add, 2 * j_add)
            if adding and j_add == PAIRS - 1:
                store(i_add)
            i, j, live = due(tick, NORMALISE_AT)
            if live and on_vector(i, j):
                normalise(nc.vector, i, 2 * j + 1)
            i, j, live = due(tick, 0)
            if live and j < len(MASK_PARTS):
                mask_scores(i, j)
            if live and j == len(MASK_PARTS) and i + 2 < TILES:
                load_scores(i + 2)
            i, j, live = due(tick, FOLD_AT)
            if live:
                fold_maxima(i, j)
            i, j, live = due(tick, MULTIPLY_AT)
            if live:
                multiply(i, 2 * j)
                multiply(i, 2 * j + 1)
                if j == 0:
                    start_total(i)
            quantised = quantise_h(quantised, issued)
            issued = project(issued, issued + min(banks, 1))
            i, j, live = due(tick, TURN_AT)
            if live:
                turn_att(i, j)
            i, j, live = due(tick, EXP_AT)
            if live:
                exponential(i, 2 * j)
                exponential(i, 2 * j + 1)
